import numpy as np
import ml_dtypes


def mxq(x, axis, fmt="e4m3"):
    dtype, down = {"e4m3": (ml_dtypes.float8_e4m3fn, 7), "e5m2": (ml_dtypes.float8_e5m2, 14)}[fmt]
    v = np.moveaxis(np.asarray(x, np.float32).astype(ml_dtypes.bfloat16).astype(np.float64), axis, -1)
    blocks = v.reshape(v.shape[:-1] + (-1, 32))
    amax = np.abs(blocks).max(-1, keepdims=True)
    byte = np.maximum(np.where(amax > 0, np.frexp(amax)[1] - 1 + 127, 0) - down, 1)
    scale = np.exp2(byte - 127.0)
    codes = (blocks / scale).astype(np.float32).astype(dtype).astype(np.float64)
    return np.moveaxis((codes * scale).reshape(v.shape), -1, axis)


WIDE = False


def mx_kscale(k):
    if not WIDE:
        return np.ones(k)
    levels = np.array([10, -10, 5, -5, 0])
    a = np.random.permutation(np.resize(levels, k // 512 * 4)).reshape(k // 512, 4)
    idx = np.arange(k)
    return np.exp2(a[idx // 512, idx % 128 // 32])


BF16 = ml_dtypes.bfloat16


def bf(x):
    return np.asarray(x, np.float32).astype(BF16)


def f64(x):
    return np.asarray(x).astype(np.float64)


B, IH, IW, H1, H2, C = 1024, 32, 32, 1024, 1024, 10
D = IH * IW
EPS = 1e-5


def batchnorm(v, gamma, beta):
    mu = v.mean(axis=0)
    var = ((v - mu) ** 2).mean(axis=0)
    return gamma * (v - mu) * (1.0 / np.sqrt(var + EPS)) + beta


def setup_inputs():
    s = mx_kscale(D)
    s = s / s.min()
    t = mx_kscale(H1)
    t = t / t.min()
    m1 = (np.resize(s, H1)[:, None] == s[None, :]).astype(np.float64)
    m2 = (np.resize(t, H2)[:, None] == t[None, :]).astype(np.float64)
    return {
        "x": bf(np.random.standard_normal((B, D)) * 8.0 / np.sqrt(D) * s[None, :]),
        "W1": bf(np.random.standard_normal((H1, D)) * 0.05 * m1),
        "g1": bf((1.0 + 0.1 * np.random.standard_normal(H1)) * 8.0 / np.sqrt(H1) * t),
        "b1": bf(np.random.standard_normal(H1) * 2.0 / np.sqrt(H1) * t),
        "W2": bf(np.random.standard_normal((H2, H1)) * 0.05 * m2),
        "g2": bf((1.0 + 0.1 * np.random.standard_normal(H2)) * 8.0 / np.sqrt(H2)),
        "b2": bf(np.random.standard_normal(H2) * 0.1),
    }


def reference(x, W1, g1, b1, W2, g2, b2):
    y1 = mxq(f64(x), 1, "e4m3") @ mxq(np.sign(f64(W1)), 1, "e4m3").T
    h1 = np.maximum(batchnorm(y1, f64(g1), f64(b1)), 0.0)
    y2 = mxq(h1, 1, "e4m3") @ mxq(np.sign(f64(W2)), 1, "e4m3").T
    return batchnorm(np.maximum(y2, 0.0), f64(g2), f64(b2))

@@ -1,0 +1,273 @@
+from contextlib import ExitStack
+
+import concourse.mybir as mybir
+from concourse.masks import make_identity
+
+F32 = mybir.dt.float32
+BF16 = mybir.dt.bfloat16
+U32 = mybir.dt.uint32
+U8 = mybir.dt.uint8
+FP8X4 = mybir.dt.float8_e4m3fn_x4
+ACT = mybir.ActivationFunctionType
+ALU = mybir.AluOpType
+
+P = 128
+SIZE = 1024
+K_PASS = 512
+PASSES = SIZE // K_PASS
+CHUNK = 2 * P
+CHUNKS = SIZE // CHUNK
+TILES = SIZE // P
+BANK = 512
+HALVES = SIZE // BANK
+EPS = 1e-5
+LEAD = 6
+AHEAD = 2
+FLOPS = 2 * 2 * SIZE * SIZE * SIZE
+
+
+def load_chunk(nc, pool, src, label, c):
+    raw = pool.tile([P, 2, SIZE], BF16, name="raw_%s%d" % (label, c))
+    nc.sync.dma_start(out=raw[:], in_=src.rearrange("(c r e) k -> c r e k", r=P, e=2)[c])
+    return raw
+
+
+def transpose_rows(nc, bank, rows, ident):
+    words = rows.bitcast(F32)
+    for w in range(BANK // P):
+        nc.tensor.transpose(bank[:, P * w : P * (w + 1)], words[:, P * w : P * (w + 1)], ident[:])
+
+
+def quantise_columns(nc, grouped, codes, scales, first, count):
+    cols = slice(first, first + count)
+    for g in range(PASSES):
+        nc.vector.quantize_mx(
+            out=codes[:, g, cols].bitcast(FP8X4),
+            scales=scales[:, g, cols],
+            in_=grouped[:, 4 * count * g : 4 * count * (g + 1)],
+        )
+
+
+def prepare_activations(nc, psum, stage, raw, ident, codes, scales, c):
+    banks = psum.tile([P, 2, BANK], F32, tag="acc", bufs=3)
+    grouped = stage.tile([P, PASSES * CHUNK * 4], BF16, tag="grouped_x", bufs=2, align_bytes=64)
+    pairs = grouped[:].bitcast(F32).rearrange("p (g c u) -> p g c u", g=PASSES, u=2)
+    for e in range(2):
+        transpose_rows(nc, banks[:, e, :], raw[:, e, :], ident)
+    for e in range(2):
+        nc.vector.tensor_copy(
+            out=pairs[:, :, P * e : P * (e + 1), :],
+            in_=banks[:, e, :].rearrange("p (g u r) -> p g r u", g=PASSES, u=2),
+        )
+    quantise_columns(nc, grouped, codes, scales, CHUNK * c, CHUNK)
+
+
+def prepare_weights(nc, psum, stage, rows, ident, codes, scales, m):
+    bank = psum.tile([P, BANK], F32, tag="tp", bufs=2)
+    grouped = stage.tile([P, PASSES * P * 4], BF16, tag="grouped_w", bufs=4, align_bytes=64)
+    transpose_rows(nc, bank, rows, ident)
+    src = bank[:].bitcast(BF16).rearrange("p (g u r e) -> p g r u e", g=PASSES, u=2, e=2)
+    dst = grouped[:].rearrange("p (g r u e) -> p g r u e", g=PASSES, u=2, e=2)
+    for g in range(PASSES):
+        nc.scalar.activation(out=dst[:, g], in_=src[:, g], func=ACT.Sign)
+    quantise_columns(nc, grouped, codes, scales, P * m, P)
+
+
+def mx_product(nc, psum, w_codes, w_scales, a_codes, a_scales, m):
+    rows = slice(P * m, P * (m + 1))
+    acc = psum.tile([P, HALVES, BANK], F32, tag="acc", bufs=3)
+    for half in range(HALVES):
+        cols = slice(BANK * half, BANK * (half + 1))
+        for g in range(PASSES):
+            nc.tensor.matmul_mx(
+                out=acc[:, half, :],
+                lhsT=w_codes[:, g, rows].bitcast(FP8X4),
+                lhsT_scale=w_scales[:, g, rows],
+                rhs=a_codes[:, g, cols].bitcast(FP8X4),
+                rhs_scale=a_scales[:, g, cols],
+                start=(g == 0),
+                stop=(g == PASSES - 1),
+            )
+    return acc
+
+
+def norm_coefficients(nc, small, values, gain, bias, neg_half):
+    stats = small.tile([P, HALVES, 6], F32, tag="stats")
+    for half in range(HALVES):
+        nc.vector.bn_stats(out=stats[:, half, :], in_=values[:, half, :])
+    mean_var = small.tile([P, 2], F32, tag="mean_var")
+    nc.vector.bn_aggr(out=mean_var[:], in_=stats[:].rearrange("p h s -> p (h s)"))
+    var_eps = small.tile([P, 1], F32, tag="var_eps")
+    nc.gpsimd.tensor_scalar(
+        out=var_eps[:], in0=mean_var[:, 1:2], scalar1=1.0, scalar2=EPS, op0=ALU.mult, op1=ALU.add
+    )
+    rstd = small.tile([P, 1], F32, tag="rstd")
+    nc.gpsimd.tensor_tensor(out=rstd[:], in0=var_eps[:], in1=neg_half[:], op=ALU.pow)
+    a = small.tile([P, 1], F32, tag="a")
+    nc.gpsimd.tensor_tensor(out=a[:], in0=gain, in1=rstd[:], op=ALU.mult)
+    mean_a = small.tile([P, 1], F32, tag="mean_a")
+    nc.gpsimd.tensor_tensor(out=mean_a[:], in0=mean_var[:, 0:1], in1=a[:], op=ALU.mult)
+    c = small.tile([P, 1], F32, tag="c")
+    nc.gpsimd.tensor_tensor(out=c[:], in0=bias, in1=mean_a[:], op=ALU.subtract)
+    return a, c
+
+
+def tile_binarylinear_pa_kernel(tc, x, W1, g1, b1, W2, g2, b2, out):
+    nc = tc.nc
+    with ExitStack() as ctx:
+        keep = ctx.enter_context(tc.tile_pool(name="keep", bufs=1))
+        stage = ctx.enter_context(tc.tile_pool(name="stage", bufs=4))
+        small = ctx.enter_context(tc.tile_pool(name="small", bufs=6))
+        psum = ctx.enter_context(tc.psum_pool(name="psum", bufs=2))
+        ctx.enter_context(tc.manual_schedule())
+
+        ident = keep.tile([P, P], F32, name="ident")
+        make_identity(nc, ident[:])
+        neg_half = keep.tile([P, 1], F32, name="neg_half")
+        nc.vector.memset(neg_half[:], -0.5)
+
+        vector_rows = keep.tile([P, CHUNK], BF16, name="vector_rows")
+        nc.vector.memset(vector_rows[:], 0.0)
+        for v, vec in enumerate((g1, b1, g2, b2)):
+            nc.scalar.dma_start(
+                out=vector_rows[CHUNKS * v : CHUNKS * (v + 1), :],
+                in_=vec.rearrange("(c n) -> c n", n=CHUNK),
+            )
+
+        raw_x = {}
+        raw_w = {}
+        raw_x[0] = load_chunk(nc, keep, x, "x", 0)
+        raw_w[0] = load_chunk(nc, keep, W1, "w", 0)
+        raw_x[1] = load_chunk(nc, keep, x, "x", 1)
+        raw_x[2] = load_chunk(nc, keep, x, "x", 2)
+        raw_w[1] = load_chunk(nc, keep, W1, "w", 1)
+        raw_x[3] = load_chunk(nc, keep, x, "x", 3)
+        raw_w[2] = load_chunk(nc, keep, W1, "w", 2)
+        raw_w[3] = load_chunk(nc, keep, W1, "w", 3)
+        for c in range(CHUNKS):
+            raw_w[CHUNKS + c] = load_chunk(nc, keep, W2, "v", c)
+
+        codes = {}
+        scales = {}
+        for label in ("x", "w1", "h1", "w2"):
+            codes[label] = keep.tile([P, PASSES, SIZE], U32, name="codes_" + label, align_bytes=64)
+            scales[label] = keep.tile([P, PASSES, SIZE], U8, name="scales_" + label, align_bytes=64)
+
+        def prepare_x(c):
+            prepare_activations(nc, psum, stage, raw_x[c], ident, codes["x"], scales["x"], c)
+
+        def prepare_w(q):
+            label = "w1" if q < TILES else "w2"
+            rows = raw_w[q // 2][:, q % 2, :]
+            prepare_weights(nc, psum, stage, rows, ident, codes[label], scales[label], q % TILES)
+
+        prepare_x(0)
+        prepare_w(0)
+        prepare_w(1)
+        prepare_x(1)
+        prepare_x(2)
+        prepare_w(2)
+        prepare_w(3)
+        prepare_x(3)
+        for q in range(4, LEAD):
+            prepare_w(q)
+
+        vector_bank = psum.tile([P, BANK], F32, tag="tp", bufs=2)
+        nc.tensor.transpose(vector_bank[:, 0:P], vector_rows[:].bitcast(F32), ident[:])
+        per_row = keep.tile([P, 4 * TILES], F32, name="per_row")
+        nc.vector.tensor_copy(out=per_row[:], in_=vector_bank[:, 0 : 4 * CHUNKS].bitcast(BF16))
+
+        h1 = [keep.tile([P, 4, SIZE], BF16, name="h1_%d" % g) for g in range(PASSES)]
+        sums = {}
+        coeff = {}
+
+        def layer1_front(m):
+            sums[m] = mx_product(nc, psum, codes["w1"], scales["w1"], codes["x"], scales["x"], m)
+            coeff[m] = norm_coefficients(
+                nc, small, sums[m], per_row[:, m : m + 1], per_row[:, TILES + m : TILES + m + 1], neg_half
+            )
+
+        for m in range(AHEAD):
+            layer1_front(m)
+        for m in range(TILES):
+            for q in range(LEAD + 2 * m, min(LEAD + 2 * m + 2, 2 * TILES)):
+                prepare_w(q)
+            if m + AHEAD < TILES:
+                layer1_front(m + AHEAD)
+            a, shift = coeff[m]
+            for half in range(HALVES):
+                nc.scalar.activation(
+                    out=h1[m // 4][:, m % 4, BANK * half : BANK * (half + 1)],
+                    in_=sums[m][:, half, :],
+                    func=ACT.Relu,
+                    bias=shift[:],
+                    scale=a[:],
+                )
+            if m % 4 == 3:
+                g = m // 4
+                for half in range(HALVES):
+                    cols = slice(BANK * half, BANK * (half + 1))
+                    grouped = stage.tile([P, BANK * 4], BF16, tag="grouped_h", bufs=2, align_bytes=64)
+                    nc.vector.tensor_copy(
+                        out=grouped[:].rearrange("p (c i t) -> p c t i", i=4, t=4),
+                        in_=h1[g][:, :, cols].rearrange("p t (c i) -> p c t i", i=4),
+                    )
+                    nc.vector.quantize_mx(
+                        out=codes["h1"][:, g, cols].bitcast(FP8X4),
+                        scales=scales["h1"][:, g, cols],
+                        in_=grouped[:],
+                    )
+
+        out_view = out.rearrange("(cb r eb) n -> cb r eb n", r=P, eb=2)
+        relu = {}
+
+        def layer2_front(m):
+            acc = mx_product(nc, psum, codes["w2"], scales["w2"], codes["h1"], scales["h1"], m)
+            relu[m] = stage.tile([P, HALVES, BANK], F32, name="relu", bufs=5)
+            for half in range(HALVES):
+                nc.scalar.activation(out=relu[m][:, half, :], in_=acc[:, half, :], func=ACT.Relu)
+            coeff[m] = norm_coefficients(
+                nc,
+                small,
+                relu[m],
+                per_row[:, 2 * TILES + m : 2 * TILES + m + 1],
+                per_row[:, 3 * TILES + m : 3 * TILES + m + 1],
+                neg_half,
+            )
+
+        for m in range(AHEAD):
+            layer2_front(m)
+        for c in range(CHUNKS):
+            for m in range(2 * c + AHEAD, min(2 * c + AHEAD + 2, TILES)):
+                layer2_front(m)
+            normed = []
+            for m in (2 * c, 2 * c + 1):
+                a, shift = coeff[m]
+                o = stage.tile([P, SIZE], F32, tag="normed", bufs=4)
+                nc.vector.tensor_scalar(
+                    out=o[:],
+                    in0=relu[m][:].rearrange("p h b -> p (h b)"),
+                    scalar1=a[:],
+                    scalar2=shift[:],
+                    op0=ALU.mult,
+                    op1=ALU.add,
+                )
+                normed.append(o)
+            for cb in range(CHUNKS):
+                bank = psum.tile([P, BANK], F32, tag="tp", bufs=2)
+                for eb in range(2):
+                    for e in range(2):
+                        w = 2 * eb + e
+                        nc.tensor.transpose(
+                            bank[:, P * w : P * (w + 1)],
+                            normed[e][:, CHUNK * cb + P * eb : CHUNK * cb + P * (eb + 1)],
+                            ident[:],
+                        )
+                rows = stage.tile([P, 2, CHUNK], F32, tag="rows", bufs=4)
+                src = bank[:].rearrange("p (eb e r) -> p eb r e", eb=2, e=2)
+                dst = rows[:].rearrange("p eb (r e) -> p eb r e", e=2)
+                if cb == CHUNKS - 1:
+                    nc.vector.tensor_copy(out=dst, in_=src)
+                else:
+                    nc.scalar.copy(out=dst, in_=src)
+                nc.sync.dma_start(out=out_view[cb][:, :, CHUNK * c : CHUNK * (c + 1)], in_=rows[:])

@@ -23,6 +23,7 @@ HALVES = SIZE // BANK
 EPS = 1e-5
 LEAD = 6
 AHEAD = 2
+STORE_LAG = 4
 FLOPS = 2 * 2 * SIZE * SIZE * SIZE
 
 
@@ -54,23 +55,23 @@ def prepare_activations(nc, psum, stage, raw, ident, codes, scales, c):
     pairs = grouped[:].bitcast(F32).rearrange("p (g c u) -> p g c u", g=PASSES, u=2)
     for e in range(2):
         transpose_rows(nc, banks[:, e, :], raw[:, e, :], ident)
-    for e in range(2):
-        nc.vector.tensor_copy(
+    for e, copy in enumerate((nc.vector.tensor_copy, nc.scalar.copy)):
+        copy(
             out=pairs[:, :, P * e : P * (e + 1), :],
             in_=banks[:, e, :].rearrange("p (g u r) -> p g r u", g=PASSES, u=2),
         )
     quantise_columns(nc, grouped, codes, scales, CHUNK * c, CHUNK)
 
 
-def prepare_weights(nc, psum, stage, rows, ident, codes, scales, m):
+def sign_rows(nc, psum, stage, rows, ident):
     bank = psum.tile([P, BANK], F32, tag="tp", bufs=2)
-    grouped = stage.tile([P, PASSES * P * 4], BF16, tag="grouped_w", bufs=4, align_bytes=64)
+    grouped = stage.tile([P, PASSES * P * 4], BF16, tag="grouped_w", bufs=6, align_bytes=64)
     transpose_rows(nc, bank, rows, ident)
     src = bank[:].bitcast(BF16).rearrange("p (g u r e) -> p g r u e", g=PASSES, u=2, e=2)
     dst = grouped[:].rearrange("p (g r u e) -> p g r u e", g=PASSES, u=2, e=2)
     for g in range(PASSES):
         nc.scalar.activation(out=dst[:, g], in_=src[:, g], func=ACT.Sign)
-    quantise_columns(nc, grouped, codes, scales, P * m, P)
+    return grouped
 
 
 def mx_product(nc, psum, w_codes, w_scales, a_codes, a_scales, m):
@@ -136,14 +137,11 @@ def tile_binarylinear_pa_kernel(tc, x, W1, g1, b1, W2, g2, b2, out):
 
         raw_x = {}
         raw_w = {}
-        raw_x[0] = load_chunk(nc, keep, x, "x", 0)
         raw_w[0] = load_chunk(nc, keep, W1, "w", 0)
-        raw_x[1] = load_chunk(nc, keep, x, "x", 1)
-        raw_x[2] = load_chunk(nc, keep, x, "x", 2)
-        raw_w[1] = load_chunk(nc, keep, W1, "w", 1)
-        raw_x[3] = load_chunk(nc, keep, x, "x", 3)
-        raw_w[2] = load_chunk(nc, keep, W1, "w", 2)
-        raw_w[3] = load_chunk(nc, keep, W1, "w", 3)
+        for c in range(CHUNKS):
+            raw_x[c] = load_chunk(nc, keep, x, "x", c)
+        for c in range(1, CHUNKS):
+            raw_w[c] = load_chunk(nc, keep, W1, "w", c)
         for c in range(CHUNKS):
             raw_w[CHUNKS + c] = load_chunk(nc, keep, W2, "v", c)
 
@@ -153,31 +151,17 @@ def tile_binarylinear_pa_kernel(tc, x, W1, g1, b1, W2, g2, b2, out):
             codes[label] = keep.tile([P, PASSES, SIZE], U32, name="codes_" + label, align_bytes=64)
             scales[label] = keep.tile([P, PASSES, SIZE], U8, name="scales_" + label, align_bytes=64)
 
-        def prepare_x(c):
-            prepare_activations(nc, psum, stage, raw_x[c], ident, codes["x"], scales["x"], c)
+        signs = {}
 
-        def prepare_w(q):
+        def take_signs(q):
+            signs[q] = sign_rows(nc, psum, stage, raw_w[q // 2][:, q % 2, :], ident)
+
+        def quantise_signs(q):
             label = "w1" if q < TILES else "w2"
-            rows = raw_w[q // 2][:, q % 2, :]
-            prepare_weights(nc, psum, stage, rows, ident, codes[label], scales[label], q % TILES)
-
-        prepare_x(0)
-        prepare_w(0)
-        prepare_w(1)
-        prepare_x(1)
-        prepare_x(2)
-        prepare_w(2)
-        prepare_w(3)
-        prepare_x(3)
-        for q in range(4, LEAD):
-            prepare_w(q)
-
-        vector_bank = psum.tile([P, BANK], F32, tag="tp", bufs=2)
-        nc.tensor.transpose(vector_bank[:, 0:P], vector_rows[:].bitcast(F32), ident[:])
-        per_row = keep.tile([P, 4 * TILES], F32, name="per_row")
-        nc.vector.tensor_copy(out=per_row[:], in_=vector_bank[:, 0 : 4 * CHUNKS].bitcast(BF16))
+            quantise_columns(nc, signs[q], codes[label], scales[label], P * (q % TILES), P)
 
         h1 = [keep.tile([P, 4, SIZE], BF16, name="h1_%d" % g) for g in range(PASSES)]
+        per_row = keep.tile([P, 4 * TILES], F32, name="per_row")
         sums = {}
         coeff = {}
 
@@ -187,13 +171,7 @@ def tile_binarylinear_pa_kernel(tc, x, W1, g1, b1, W2, g2, b2, out):
                 nc, small, sums[m], per_row[:, m : m + 1], per_row[:, TILES + m : TILES + m + 1], neg_half
             )
 
-        for m in range(AHEAD):
-            layer1_front(m)
-        for m in range(TILES):
-            for q in range(LEAD + 2 * m, min(LEAD + 2 * m + 2, 2 * TILES)):
-                prepare_w(q)
-            if m + AHEAD < TILES:
-                layer1_front(m + AHEAD)
+        def layer1_normalise(m):
             a, shift = coeff[m]
             for half in range(HALVES):
                 nc.scalar.activation(
@@ -203,29 +181,64 @@ def tile_binarylinear_pa_kernel(tc, x, W1, g1, b1, W2, g2, b2, out):
                     bias=shift[:],
                     scale=a[:],
                 )
+
+        def quantise_h1(g):
+            for half in range(HALVES):
+                cols = slice(BANK * half, BANK * (half + 1))
+                grouped = stage.tile([P, BANK * 4], BF16, tag="grouped_h", bufs=2, align_bytes=64)
+                nc.vector.tensor_copy(
+                    out=grouped[:].rearrange("p (c i t) -> p c t i", i=4, t=4),
+                    in_=h1[g][:, :, cols].rearrange("p t (c i) -> p c t i", i=4),
+                )
+                nc.vector.quantize_mx(
+                    out=codes["h1"][:, g, cols].bitcast(FP8X4),
+                    scales=scales["h1"][:, g, cols],
+                    in_=grouped[:],
+                )
+
+        take_signs(0)
+        take_signs(1)
+        for c in range(CHUNKS):
+            prepare_activations(nc, psum, stage, raw_x[c], ident, codes["x"], scales["x"], c)
+        quantise_signs(0)
+        quantise_signs(1)
+
+        vector_bank = psum.tile([P, BANK], F32, tag="tp", bufs=2)
+        nc.tensor.transpose(vector_bank[:, 0:P], vector_rows[:].bitcast(F32), ident[:])
+        nc.vector.tensor_copy(out=per_row[:], in_=vector_bank[:, 0 : 4 * CHUNKS].bitcast(BF16))
+
+        take_signs(2)
+        take_signs(3)
+        take_signs(4)
+        layer1_front(0)
+        take_signs(5)
+        layer1_front(1)
+        for q in range(2, LEAD):
+            quantise_signs(q)
+
+        for m in range(TILES):
+            take_signs(LEAD + m)
+            quantise_signs(LEAD + m)
+            if m + AHEAD < TILES:
+                layer1_front(m + AHEAD)
+            layer1_normalise(m)
             if m % 4 == 3:
-                g = m // 4
-                for half in range(HALVES):
-                    cols = slice(BANK * half, BANK * (half + 1))
-                    grouped = stage.tile([P, BANK * 4], BF16, tag="grouped_h", bufs=2, align_bytes=64)
-                    nc.vector.tensor_copy(
-                        out=grouped[:].rearrange("p (c i t) -> p c t i", i=4, t=4),
-                        in_=h1[g][:, :, cols].rearrange("p t (c i) -> p c t i", i=4),
-                    )
-                    nc.vector.quantize_mx(
-                        out=codes["h1"][:, g, cols].bitcast(FP8X4),
-                        scales=scales["h1"][:, g, cols],
-                        in_=grouped[:],
-                    )
+                quantise_h1(m // 4)
+        for q in range(LEAD + TILES, 2 * TILES):
+            take_signs(q)
+            quantise_signs(q)
 
         out_view = out.rearrange("(cb r eb) n -> cb r eb n", r=P, eb=2)
         relu = {}
+        normed = {}
 
-        def layer2_front(m):
-            acc = mx_product(nc, psum, codes["w2"], scales["w2"], codes["h1"], scales["h1"], m)
-            relu[m] = stage.tile([P, HALVES, BANK], F32, name="relu", bufs=5)
+        def layer2_product(m):
+            sums[m] = mx_product(nc, psum, codes["w2"], scales["w2"], codes["h1"], scales["h1"], m)
+
+        def layer2_relu(m):
+            relu[m] = stage.tile([P, HALVES, BANK], F32, name="relu", bufs=4)
             for half in range(HALVES):
-                nc.scalar.activation(out=relu[m][:, half, :], in_=acc[:, half, :], func=ACT.Relu)
+                nc.scalar.activation(out=relu[m][:, half, :], in_=sums[m][:, half, :], func=ACT.Relu)
             coeff[m] = norm_coefficients(
                 nc,
                 small,
@@ -235,39 +248,45 @@ def tile_binarylinear_pa_kernel(tc, x, W1, g1, b1, W2, g2, b2, out):
                 neg_half,
             )
 
-        for m in range(AHEAD):
-            layer2_front(m)
-        for c in range(CHUNKS):
-            for m in range(2 * c + AHEAD, min(2 * c + AHEAD + 2, TILES)):
-                layer2_front(m)
-            normed = []
-            for m in (2 * c, 2 * c + 1):
-                a, shift = coeff[m]
-                o = stage.tile([P, SIZE], F32, tag="normed", bufs=4)
-                nc.vector.tensor_scalar(
-                    out=o[:],
-                    in0=relu[m][:].rearrange("p h b -> p (h b)"),
-                    scalar1=a[:],
-                    scalar2=shift[:],
-                    op0=ALU.mult,
-                    op1=ALU.add,
-                )
-                normed.append(o)
-            for cb in range(CHUNKS):
-                bank = psum.tile([P, BANK], F32, tag="tp", bufs=2)
-                for eb in range(2):
-                    for e in range(2):
-                        w = 2 * eb + e
-                        nc.tensor.transpose(
-                            bank[:, P * w : P * (w + 1)],
-                            normed[e][:, CHUNK * cb + P * eb : CHUNK * cb + P * (eb + 1)],
-                            ident[:],
-                        )
-                rows = stage.tile([P, 2, CHUNK], F32, tag="rows", bufs=4)
-                src = bank[:].rearrange("p (eb e r) -> p eb r e", eb=2, e=2)
-                dst = rows[:].rearrange("p eb (r e) -> p eb r e", e=2)
-                if cb == CHUNKS - 1:
-                    nc.vector.tensor_copy(out=dst, in_=src)
-                else:
-                    nc.scalar.copy(out=dst, in_=src)
-                nc.sync.dma_start(out=out_view[cb][:, :, CHUNK * c : CHUNK * (c + 1)], in_=rows[:])
+        def layer2_normalise(m):
+            a, shift = coeff[m]
+            normed[m] = stage.tile([P, SIZE], F32, name="normed", bufs=5)
+            nc.vector.tensor_scalar(
+                out=normed[m][:],
+                in0=relu[m][:].rearrange("p h b -> p (h b)"),
+                scalar1=a[:],
+                scalar2=shift[:],
+                op0=ALU.mult,
+                op1=ALU.add,
+            )
+
+        def store_block(c, cb, copy):
+            bank = psum.tile([P, BANK], F32, tag="tp", bufs=2)
+            for eb in range(2):
+                for e in range(2):
+                    w = 2 * eb + e
+                    nc.tensor.transpose(
+                        bank[:, P * w : P * (w + 1)],
+                        normed[2 * c + e][:, CHUNK * cb + P * eb : CHUNK * cb + P * (eb + 1)],
+                        ident[:],
+                    )
+            rows = stage.tile([P, 2, CHUNK], F32, tag="rows", bufs=4)
+            copy(
+                out=rows[:].rearrange("p eb (j e) -> p eb j e", e=2),
+                in_=bank[:].rearrange("p (eb e j) -> p eb j e", eb=2, e=2),
+            )
+            nc.sync.dma_start(out=out_view[cb][:, :, CHUNK * c : CHUNK * (c + 1)], in_=rows[:])
+
+        layer2_product(0)
+        for i in range(TILES + STORE_LAG):
+            if 2 <= i < TILES + 2:
+                layer2_normalise(i - 2)
+            if i < TILES:
+                layer2_relu(i)
+            if i >= STORE_LAG:
+                c = (i - STORE_LAG) // 2
+                cb = 2 * ((i - STORE_LAG) % 2)
+                store_block(c, cb, nc.scalar.copy)
+                store_block(c, cb + 1, nc.vector.tensor_copy if i % 2 == 1 else nc.scalar.copy)
+            if i + 1 < TILES:
+                layer2_product(i + 1)

@@ -50,21 +50,20 @@ def quantise_columns(nc, grouped, codes, scales, first, count):
 
 
 def prepare_activations(nc, psum, stage, raw, ident, codes, scales, c):
-    banks = psum.tile([P, 2, BANK], F32, tag="acc", bufs=3)
     grouped = stage.tile([P, PASSES * CHUNK * 4], BF16, tag="grouped_x", bufs=2, align_bytes=64)
     pairs = grouped[:].bitcast(F32).rearrange("p (g c u) -> p g c u", g=PASSES, u=2)
-    for e in range(2):
-        transpose_rows(nc, banks[:, e, :], raw[:, e, :], ident)
     for e, copy in enumerate((nc.vector.tensor_copy, nc.scalar.copy)):
+        bank = psum.tile([P, BANK], F32, tag="bank")
+        transpose_rows(nc, bank, raw[:, e, :], ident)
         copy(
             out=pairs[:, :, P * e : P * (e + 1), :],
-            in_=banks[:, e, :].rearrange("p (g u r) -> p g r u", g=PASSES, u=2),
+            in_=bank[:].rearrange("p (g u r) -> p g r u", g=PASSES, u=2),
         )
     quantise_columns(nc, grouped, codes, scales, CHUNK * c, CHUNK)
 
 
 def sign_rows(nc, psum, stage, rows, ident):
-    bank = psum.tile([P, BANK], F32, tag="tp", bufs=2)
+    bank = psum.tile([P, BANK], F32, tag="bank")
     grouped = stage.tile([P, PASSES * P * 4], BF16, tag="grouped_w", bufs=6, align_bytes=64)
     transpose_rows(nc, bank, rows, ident)
     src = bank[:].bitcast(BF16).rearrange("p (g u r e) -> p g r u e", g=PASSES, u=2, e=2)
@@ -76,12 +75,14 @@ def sign_rows(nc, psum, stage, rows, ident):
 
 def mx_product(nc, psum, w_codes, w_scales, a_codes, a_scales, m):
     rows = slice(P * m, P * (m + 1))
-    acc = psum.tile([P, HALVES, BANK], F32, tag="acc", bufs=3)
+    halves = []
     for half in range(HALVES):
         cols = slice(BANK * half, BANK * (half + 1))
+        acc = psum.tile([P, BANK], F32, tag="bank")
+        halves.append(acc)
         for g in range(PASSES):
             nc.tensor.matmul_mx(
-                out=acc[:, half, :],
+                out=acc[:],
                 lhsT=w_codes[:, g, rows].bitcast(FP8X4),
                 lhsT_scale=w_scales[:, g, rows],
                 rhs=a_codes[:, g, cols].bitcast(FP8X4),
@@ -89,13 +90,13 @@ def mx_product(nc, psum, w_codes, w_scales, a_codes, a_scales, m):
                 start=(g == 0),
                 stop=(g == PASSES - 1),
             )
-    return acc
+    return halves
 
 
-def norm_coefficients(nc, small, values, gain, bias, neg_half):
+def norm_coefficients(nc, small, halves, gain_pair, bias, neg_half):
     stats = small.tile([P, HALVES, 6], F32, tag="stats")
     for half in range(HALVES):
-        nc.vector.bn_stats(out=stats[:, half, :], in_=values[:, half, :])
+        nc.vector.bn_stats(out=stats[:, half, :], in_=halves[half])
     mean_var = small.tile([P, 2], F32, tag="mean_var")
     nc.vector.bn_aggr(out=mean_var[:], in_=stats[:].rearrange("p h s -> p (h s)"))
     var_eps = small.tile([P, 1], F32, tag="var_eps")
@@ -104,13 +105,15 @@ def norm_coefficients(nc, small, values, gain, bias, neg_half):
     )
     rstd = small.tile([P, 1], F32, tag="rstd")
     nc.gpsimd.tensor_tensor(out=rstd[:], in0=var_eps[:], in1=neg_half[:], op=ALU.pow)
-    a = small.tile([P, 1], F32, tag="a")
-    nc.gpsimd.tensor_tensor(out=a[:], in0=gain, in1=rstd[:], op=ALU.mult)
-    mean_a = small.tile([P, 1], F32, tag="mean_a")
-    nc.gpsimd.tensor_tensor(out=mean_a[:], in0=mean_var[:, 0:1], in1=a[:], op=ALU.mult)
+    a_pair = small.tile([P, 2], F32, tag="a_pair")
+    nc.gpsimd.tensor_scalar(
+        out=a_pair[:], in0=gain_pair, scalar1=rstd[:], scalar2=0.0, op0=ALU.mult, op1=ALU.add
+    )
     c = small.tile([P, 1], F32, tag="c")
-    nc.gpsimd.tensor_tensor(out=c[:], in0=bias, in1=mean_a[:], op=ALU.subtract)
-    return a, c
+    nc.gpsimd.tensor_scalar(
+        out=c[:], in0=mean_var[:, 0:1], scalar1=a_pair[:, 1:2], scalar2=bias, op0=ALU.mult, op1=ALU.add
+    )
+    return a_pair[:, 0:1], c[:]
 
 
 def tile_binarylinear_pa_kernel(tc, x, W1, g1, b1, W2, g2, b2, out):
@@ -119,8 +122,7 @@ def tile_binarylinear_pa_kernel(tc, x, W1, g1, b1, W2, g2, b2, out):
         keep = ctx.enter_context(tc.tile_pool(name="keep", bufs=1))
         stage = ctx.enter_context(tc.tile_pool(name="stage", bufs=4))
         small = ctx.enter_context(tc.tile_pool(name="small", bufs=6))
-        psum = ctx.enter_context(tc.psum_pool(name="psum", bufs=2))
-        ctx.enter_context(tc.manual_schedule())
+        psum = ctx.enter_context(tc.psum_pool(name="psum", bufs=8))
 
         ident = keep.tile([P, P], F32, name="ident")
         make_identity(nc, ident[:])
@@ -129,7 +131,7 @@ def tile_binarylinear_pa_kernel(tc, x, W1, g1, b1, W2, g2, b2, out):
 
         vector_rows = keep.tile([P, CHUNK], BF16, name="vector_rows")
         nc.vector.memset(vector_rows[:], 0.0)
-        for v, vec in enumerate((g1, b1, g2, b2)):
+        for v, vec in enumerate((g1, g2, b1, b2)):
             nc.scalar.dma_start(
                 out=vector_rows[CHUNKS * v : CHUNKS * (v + 1), :],
                 in_=vec.rearrange("(c n) -> c n", n=CHUNK),
@@ -161,14 +163,15 @@ def tile_binarylinear_pa_kernel(tc, x, W1, g1, b1, W2, g2, b2, out):
             quantise_columns(nc, signs[q], codes[label], scales[label], P * (q % TILES), P)
 
         h1 = [keep.tile([P, 4, SIZE], BF16, name="h1_%d" % g) for g in range(PASSES)]
-        per_row = keep.tile([P, 4 * TILES], F32, name="per_row")
+        gain_pairs = keep.tile([P, 2 * TILES, 2], F32, name="gain_pairs")
+        biases = keep.tile([P, 2 * TILES], F32, name="biases")
         sums = {}
         coeff = {}
 
         def layer1_front(m):
             sums[m] = mx_product(nc, psum, codes["w1"], scales["w1"], codes["x"], scales["x"], m)
             coeff[m] = norm_coefficients(
-                nc, small, sums[m], per_row[:, m : m + 1], per_row[:, TILES + m : TILES + m + 1], neg_half
+                nc, small, sums[m], gain_pairs[:, m, :], biases[:, m : m + 1], neg_half
             )
 
         def layer1_normalise(m):
@@ -176,10 +179,10 @@ def tile_binarylinear_pa_kernel(tc, x, W1, g1, b1, W2, g2, b2, out):
             for half in range(HALVES):
                 nc.scalar.activation(
                     out=h1[m // 4][:, m % 4, BANK * half : BANK * (half + 1)],
-                    in_=sums[m][:, half, :],
+                    in_=sums[m][half][:],
                     func=ACT.Relu,
-                    bias=shift[:],
-                    scale=a[:],
+                    bias=shift,
+                    scale=a,
                 )
 
         def quantise_h1(g):
@@ -203,9 +206,12 @@ def tile_binarylinear_pa_kernel(tc, x, W1, g1, b1, W2, g2, b2, out):
         quantise_signs(0)
         quantise_signs(1)
 
-        vector_bank = psum.tile([P, BANK], F32, tag="tp", bufs=2)
+        vector_bank = psum.tile([P, BANK], F32, tag="bank")
         nc.tensor.transpose(vector_bank[:, 0:P], vector_rows[:].bitcast(F32), ident[:])
-        nc.vector.tensor_copy(out=per_row[:], in_=vector_bank[:, 0 : 4 * CHUNKS].bitcast(BF16))
+        gains = vector_bank[:, 0 : 2 * CHUNKS].bitcast(BF16)
+        nc.vector.tensor_copy(out=gain_pairs[:, :, 0], in_=gains)
+        nc.vector.tensor_scalar_mul(out=gain_pairs[:, :, 1], in0=gains, scalar1=-1.0)
+        nc.vector.tensor_copy(out=biases[:], in_=vector_bank[:, 2 * CHUNKS : 4 * CHUNKS].bitcast(BF16))
 
         take_signs(2)
         take_signs(3)
@@ -238,13 +244,13 @@ def tile_binarylinear_pa_kernel(tc, x, W1, g1, b1, W2, g2, b2, out):
         def layer2_relu(m):
             relu[m] = stage.tile([P, HALVES, BANK], F32, name="relu", bufs=4)
             for half in range(HALVES):
-                nc.scalar.activation(out=relu[m][:, half, :], in_=sums[m][:, half, :], func=ACT.Relu)
+                nc.scalar.activation(out=relu[m][:, half, :], in_=sums[m][half][:], func=ACT.Relu)
             coeff[m] = norm_coefficients(
                 nc,
                 small,
-                relu[m],
-                per_row[:, 2 * TILES + m : 2 * TILES + m + 1],
-                per_row[:, 3 * TILES + m : 3 * TILES + m + 1],
+                [relu[m][:, half, :] for half in range(HALVES)],
+                gain_pairs[:, TILES + m, :],
+                biases[:, TILES + m : TILES + m + 1],
                 neg_half,
             )
 
@@ -254,14 +260,14 @@ def tile_binarylinear_pa_kernel(tc, x, W1, g1, b1, W2, g2, b2, out):
             nc.vector.tensor_scalar(
                 out=normed[m][:],
                 in0=relu[m][:].rearrange("p h b -> p (h b)"),
-                scalar1=a[:],
-                scalar2=shift[:],
+                scalar1=a,
+                scalar2=shift,
                 op0=ALU.mult,
                 op1=ALU.add,
             )
 
         def store_block(c, cb, copy):
-            bank = psum.tile([P, BANK], F32, tag="tp", bufs=2)
+            bank = psum.tile([P, BANK], F32, tag="bank")
             for eb in range(2):
                 for e in range(2):
                     w = 2 * eb + e

@@ -93,18 +93,14 @@ def mx_product(nc, psum, w_codes, w_scales, a_codes, a_scales, m):
     return halves
 
 
-def norm_coefficients(nc, small, halves, gain_pair, bias, neg_half):
+def norm_coefficients(nc, small, halves, gain_pair, bias, eps):
     stats = small.tile([P, HALVES, 6], F32, tag="stats")
     for half in range(HALVES):
         nc.vector.bn_stats(out=stats[:, half, :], in_=halves[half])
     mean_var = small.tile([P, 2], F32, tag="mean_var")
     nc.vector.bn_aggr(out=mean_var[:], in_=stats[:].rearrange("p h s -> p (h s)"))
-    var_eps = small.tile([P, 1], F32, tag="var_eps")
-    nc.gpsimd.tensor_scalar(
-        out=var_eps[:], in0=mean_var[:, 1:2], scalar1=1.0, scalar2=EPS, op0=ALU.mult, op1=ALU.add
-    )
     rstd = small.tile([P, 1], F32, tag="rstd")
-    nc.gpsimd.tensor_tensor(out=rstd[:], in0=var_eps[:], in1=neg_half[:], op=ALU.pow)
+    nc.scalar.activation(out=rstd[:], in_=mean_var[:, 1:2], func=ACT.Abs_reciprocal_sqrt, bias=eps[:])
     a_pair = small.tile([P, 2], F32, tag="a_pair")
     nc.gpsimd.tensor_scalar(
         out=a_pair[:], in0=gain_pair, scalar1=rstd[:], scalar2=0.0, op0=ALU.mult, op1=ALU.add
@@ -126,8 +122,8 @@ def tile_binarylinear_pa_kernel(tc, x, W1, g1, b1, W2, g2, b2, out):
 
         ident = keep.tile([P, P], F32, name="ident")
         make_identity(nc, ident[:])
-        neg_half = keep.tile([P, 1], F32, name="neg_half")
-        nc.vector.memset(neg_half[:], -0.5)
+        eps = keep.tile([P, 1], F32, name="eps")
+        nc.vector.memset(eps[:], EPS)
 
         vector_rows = keep.tile([P, CHUNK], BF16, name="vector_rows")
         nc.vector.memset(vector_rows[:], 0.0)
@@ -171,7 +167,7 @@ def tile_binarylinear_pa_kernel(tc, x, W1, g1, b1, W2, g2, b2, out):
         def layer1_front(m):
             sums[m] = mx_product(nc, psum, codes["w1"], scales["w1"], codes["x"], scales["x"], m)
             coeff[m] = norm_coefficients(
-                nc, small, sums[m], gain_pairs[:, m, :], biases[:, m : m + 1], neg_half
+                nc, small, sums[m], gain_pairs[:, m, :], biases[:, m : m + 1], eps
             )
 
         def layer1_normalise(m):
@@ -251,7 +247,7 @@ def tile_binarylinear_pa_kernel(tc, x, W1, g1, b1, W2, g2, b2, out):
                 [relu[m][:, half, :] for half in range(HALVES)],
                 gain_pairs[:, TILES + m, :],
                 biases[:, TILES + m : TILES + m + 1],
-                neg_half,
+                eps,
             )
 
         def layer2_normalise(m):

@@ -23,6 +23,7 @@ HALVES = SIZE // BANK
 EPS = 1e-5
 LEAD = 6
 AHEAD = 2
+NORM_LAG = 2
 STORE_LAG = 4
 FLOPS = 2 * 2 * SIZE * SIZE * SIZE
 
@@ -209,14 +210,11 @@ def tile_binarylinear_pa_kernel(tc, x, W1, g1, b1, W2, g2, b2, out):
         nc.vector.tensor_scalar_mul(out=gain_pairs[:, :, 1], in0=gains, scalar1=-1.0)
         nc.vector.tensor_copy(out=biases[:], in_=vector_bank[:, 2 * CHUNKS : 4 * CHUNKS].bitcast(BF16))
 
-        take_signs(2)
-        take_signs(3)
-        take_signs(4)
-        layer1_front(0)
-        take_signs(5)
-        layer1_front(1)
         for q in range(2, LEAD):
+            take_signs(q)
             quantise_signs(q)
+        for m in range(AHEAD):
+            layer1_front(m)
 
         for m in range(TILES):
             take_signs(LEAD + m)
@@ -262,7 +260,7 @@ def tile_binarylinear_pa_kernel(tc, x, W1, g1, b1, W2, g2, b2, out):
                 op1=ALU.add,
             )
 
-        def store_block(c, cb, copy):
+        def store_block(c, cb):
             bank = psum.tile([P, BANK], F32, tag="bank")
             for eb in range(2):
                 for e in range(2):
@@ -273,6 +271,7 @@ def tile_binarylinear_pa_kernel(tc, x, W1, g1, b1, W2, g2, b2, out):
                         ident[:],
                     )
             rows = stage.tile([P, 2, CHUNK], F32, tag="rows", bufs=4)
+            copy = nc.vector.tensor_copy if cb == CHUNKS - 1 else nc.scalar.copy
             copy(
                 out=rows[:].rearrange("p eb (j e) -> p eb j e", e=2),
                 in_=bank[:].rearrange("p (eb e j) -> p eb j e", eb=2, e=2),
@@ -281,14 +280,14 @@ def tile_binarylinear_pa_kernel(tc, x, W1, g1, b1, W2, g2, b2, out):
 
         layer2_product(0)
         for i in range(TILES + STORE_LAG):
-            if 2 <= i < TILES + 2:
-                layer2_normalise(i - 2)
+            if NORM_LAG <= i < TILES + NORM_LAG:
+                layer2_normalise(i - NORM_LAG)
             if i < TILES:
                 layer2_relu(i)
             if i >= STORE_LAG:
                 c = (i - STORE_LAG) // 2
                 cb = 2 * ((i - STORE_LAG) % 2)
-                store_block(c, cb, nc.scalar.copy)
-                store_block(c, cb + 1, nc.vector.tensor_copy if i % 2 == 1 else nc.scalar.copy)
+                store_block(c, cb)
+                store_block(c, cb + 1)
             if i + 1 < TILES:
                 layer2_product(i + 1)

@@ -94,23 +94,23 @@ def mx_product(nc, psum, w_codes, w_scales, a_codes, a_scales, m):
     return halves
 
 
-def norm_coefficients(nc, small, halves, gain_pair, bias, eps):
+def norm_coefficients(nc, small, halves, gain, neg_gain, bias, eps):
     stats = small.tile([P, HALVES, 6], F32, tag="stats")
     for half in range(HALVES):
         nc.vector.bn_stats(out=stats[:, half, :], in_=halves[half])
     mean_var = small.tile([P, 2], F32, tag="mean_var")
     nc.vector.bn_aggr(out=mean_var[:], in_=stats[:].rearrange("p h s -> p (h s)"))
+    neg_gain_mean = small.tile([P, 1], F32, tag="neg_gain_mean")
+    nc.gpsimd.tensor_tensor(out=neg_gain_mean[:], in0=mean_var[:, 0:1], in1=neg_gain, op=ALU.mult)
     rstd = small.tile([P, 1], F32, tag="rstd")
     nc.scalar.activation(out=rstd[:], in_=mean_var[:, 1:2], func=ACT.Abs_reciprocal_sqrt, bias=eps[:])
-    a_pair = small.tile([P, 2], F32, tag="a_pair")
-    nc.gpsimd.tensor_scalar(
-        out=a_pair[:], in0=gain_pair, scalar1=rstd[:], scalar2=0.0, op0=ALU.mult, op1=ALU.add
-    )
+    a = small.tile([P, 1], F32, tag="a")
+    nc.vector.tensor_tensor(out=a[:], in0=gain, in1=rstd[:], op=ALU.mult)
     c = small.tile([P, 1], F32, tag="c")
     nc.gpsimd.tensor_scalar(
-        out=c[:], in0=mean_var[:, 0:1], scalar1=a_pair[:, 1:2], scalar2=bias, op0=ALU.mult, op1=ALU.add
+        out=c[:], in0=neg_gain_mean[:], scalar1=rstd[:], scalar2=bias, op0=ALU.mult, op1=ALU.add
     )
-    return a_pair[:, 0:1], c[:]
+    return a[:], c[:]
 
 
 def tile_binarylinear_pa_kernel(tc, x, W1, g1, b1, W2, g2, b2, out):
@@ -160,7 +160,8 @@ def tile_binarylinear_pa_kernel(tc, x, W1, g1, b1, W2, g2, b2, out):
             quantise_columns(nc, signs[q], codes[label], scales[label], P * (q % TILES), P)
 
         h1 = [keep.tile([P, 4, SIZE], BF16, name="h1_%d" % g) for g in range(PASSES)]
-        gain_pairs = keep.tile([P, 2 * TILES, 2], F32, name="gain_pairs")
+        gains = keep.tile([P, 2 * TILES], F32, name="gains")
+        neg_gains = keep.tile([P, 2 * TILES], F32, name="neg_gains")
         biases = keep.tile([P, 2 * TILES], F32, name="biases")
         sums = {}
         coeff = {}
@@ -168,7 +169,7 @@ def tile_binarylinear_pa_kernel(tc, x, W1, g1, b1, W2, g2, b2, out):
         def layer1_front(m):
             sums[m] = mx_product(nc, psum, codes["w1"], scales["w1"], codes["x"], scales["x"], m)
             coeff[m] = norm_coefficients(
-                nc, small, sums[m], gain_pairs[:, m, :], biases[:, m : m + 1], eps
+                nc, small, sums[m], gains[:, m : m + 1], neg_gains[:, m : m + 1], biases[:, m : m + 1], eps
             )
 
         def layer1_normalise(m):
@@ -205,9 +206,10 @@ def tile_binarylinear_pa_kernel(tc, x, W1, g1, b1, W2, g2, b2, out):
 
         vector_bank = psum.tile([P, BANK], F32, tag="bank")
         nc.tensor.transpose(vector_bank[:, 0:P], vector_rows[:].bitcast(F32), ident[:])
-        gains = vector_bank[:, 0 : 2 * CHUNKS].bitcast(BF16)
-        nc.vector.tensor_copy(out=gain_pairs[:, :, 0], in_=gains)
-        nc.vector.tensor_scalar_mul(out=gain_pairs[:, :, 1], in0=gains, scalar1=-1.0)
+        nc.vector.tensor_copy(out=gains[:], in_=vector_bank[:, 0 : 2 * CHUNKS].bitcast(BF16))
+        nc.vector.tensor_scalar_mul(
+            out=neg_gains[:], in0=vector_bank[:, 0 : 2 * CHUNKS].bitcast(BF16), scalar1=-1.0
+        )
         nc.vector.tensor_copy(out=biases[:], in_=vector_bank[:, 2 * CHUNKS : 4 * CHUNKS].bitcast(BF16))
 
         for q in range(2, LEAD):
@@ -243,7 +245,8 @@ def tile_binarylinear_pa_kernel(tc, x, W1, g1, b1, W2, g2, b2, out):
                 nc,
                 small,
                 [relu[m][:, half, :] for half in range(HALVES)],
-                gain_pairs[:, TILES + m, :],
+                gains[:, TILES + m : TILES + m + 1],
+                neg_gains[:, TILES + m : TILES + m + 1],
                 biases[:, TILES + m : TILES + m + 1],
                 eps,
             )

@@ -21,10 +21,7 @@ TILES = SIZE // P
 BANK = 512
 HALVES = SIZE // BANK
 EPS = 1e-5
-LEAD = 6
-AHEAD = 2
-NORM_LAG = 2
-STORE_LAG = 4
+TINY = 2.0**-126
 FLOPS = 2 * 2 * SIZE * SIZE * SIZE
 
 
@@ -37,80 +34,9 @@ def load_chunk(nc, pool, src, label, c):
 def transpose_rows(nc, bank, rows, ident):
     words = rows.bitcast(F32)
     for w in range(BANK // P):
-        nc.tensor.transpose(bank[:, P * w : P * (w + 1)], words[:, P * w : P * (w + 1)], ident[:])
-
-
-def quantise_columns(nc, grouped, codes, scales, first, count):
-    cols = slice(first, first + count)
-    for g in range(PASSES):
-        nc.vector.quantize_mx(
-            out=codes[:, g, cols].bitcast(FP8X4),
-            scales=scales[:, g, cols],
-            in_=grouped[:, 4 * count * g : 4 * count * (g + 1)],
-        )
-
-
-def prepare_activations(nc, psum, stage, raw, ident, codes, scales, c):
-    grouped = stage.tile([P, PASSES * CHUNK * 4], BF16, tag="grouped_x", bufs=2, align_bytes=64)
-    pairs = grouped[:].bitcast(F32).rearrange("p (g c u) -> p g c u", g=PASSES, u=2)
-    for e, copy in enumerate((nc.vector.tensor_copy, nc.scalar.copy)):
-        bank = psum.tile([P, BANK], F32, tag="bank")
-        transpose_rows(nc, bank, raw[:, e, :], ident)
-        copy(
-            out=pairs[:, :, P * e : P * (e + 1), :],
-            in_=bank[:].rearrange("p (g u r) -> p g r u", g=PASSES, u=2),
-        )
-    quantise_columns(nc, grouped, codes, scales, CHUNK * c, CHUNK)
-
-
-def sign_rows(nc, psum, stage, rows, ident):
-    bank = psum.tile([P, BANK], F32, tag="bank")
-    grouped = stage.tile([P, PASSES * P * 4], BF16, tag="grouped_w", bufs=6, align_bytes=64)
-    transpose_rows(nc, bank, rows, ident)
-    src = bank[:].bitcast(BF16).rearrange("p (g u r e) -> p g r u e", g=PASSES, u=2, e=2)
-    dst = grouped[:].rearrange("p (g r u e) -> p g r u e", g=PASSES, u=2, e=2)
-    for g in range(PASSES):
-        nc.scalar.activation(out=dst[:, g], in_=src[:, g], func=ACT.Sign)
-    return grouped
-
-
-def mx_product(nc, psum, w_codes, w_scales, a_codes, a_scales, m):
-    rows = slice(P * m, P * (m + 1))
-    halves = []
-    for half in range(HALVES):
-        cols = slice(BANK * half, BANK * (half + 1))
-        acc = psum.tile([P, BANK], F32, tag="bank")
-        halves.append(acc)
-        for g in range(PASSES):
-            nc.tensor.matmul_mx(
-                out=acc[:],
-                lhsT=w_codes[:, g, rows].bitcast(FP8X4),
-                lhsT_scale=w_scales[:, g, rows],
-                rhs=a_codes[:, g, cols].bitcast(FP8X4),
-                rhs_scale=a_scales[:, g, cols],
-                start=(g == 0),
-                stop=(g == PASSES - 1),
-            )
-    return halves
-
-
-def norm_coefficients(nc, small, halves, gain, neg_gain, bias, eps):
-    stats = small.tile([P, HALVES, 6], F32, tag="stats")
-    for half in range(HALVES):
-        nc.vector.bn_stats(out=stats[:, half, :], in_=halves[half])
-    mean_var = small.tile([P, 2], F32, tag="mean_var")
-    nc.vector.bn_aggr(out=mean_var[:], in_=stats[:].rearrange("p h s -> p (h s)"))
-    neg_gain_mean = small.tile([P, 1], F32, tag="neg_gain_mean")
-    nc.gpsimd.tensor_tensor(out=neg_gain_mean[:], in0=mean_var[:, 0:1], in1=neg_gain, op=ALU.mult)
-    rstd = small.tile([P, 1], F32, tag="rstd")
-    nc.scalar.activation(out=rstd[:], in_=mean_var[:, 1:2], func=ACT.Abs_reciprocal_sqrt, bias=eps[:])
-    a = small.tile([P, 1], F32, tag="a")
-    nc.vector.tensor_tensor(out=a[:], in0=gain, in1=rstd[:], op=ALU.mult)
-    c = small.tile([P, 1], F32, tag="c")
-    nc.gpsimd.tensor_scalar(
-        out=c[:], in0=neg_gain_mean[:], scalar1=rstd[:], scalar2=bias, op0=ALU.mult, op1=ALU.add
-    )
-    return a[:], c[:]
+        g, u = w // 2, w % 2
+        block = PASSES * u + g
+        nc.tensor.transpose(bank[:, P * block : P * (block + 1)], words[:, P * w : P * (w + 1)], ident[:])
 
 
 def tile_binarylinear_pa_kernel(tc, x, W1, g1, b1, W2, g2, b2, out):
@@ -120,19 +46,21 @@ def tile_binarylinear_pa_kernel(tc, x, W1, g1, b1, W2, g2, b2, out):
         stage = ctx.enter_context(tc.tile_pool(name="stage", bufs=4))
         small = ctx.enter_context(tc.tile_pool(name="small", bufs=6))
         psum = ctx.enter_context(tc.psum_pool(name="psum", bufs=8))
+        ctx.enter_context(tc.manual_schedule())
 
-        ident = keep.tile([P, P], F32, name="ident")
-        make_identity(nc, ident[:])
         eps = keep.tile([P, 1], F32, name="eps")
         nc.vector.memset(eps[:], EPS)
-
         vector_rows = keep.tile([P, CHUNK], BF16, name="vector_rows")
         nc.vector.memset(vector_rows[:], 0.0)
+        ident = keep.tile([P, P], F32, name="ident")
+        make_identity(nc, ident[:])
         for v, vec in enumerate((g1, g2, b1, b2)):
             nc.scalar.dma_start(
                 out=vector_rows[CHUNKS * v : CHUNKS * (v + 1), :],
                 in_=vec.rearrange("(c n) -> c n", n=CHUNK),
             )
+        warm = keep.tile([P, 1], F32, name="warm")
+        nc.scalar.activation(out=warm[:], in_=eps[:], func=ACT.Abs_reciprocal_sqrt)
 
         raw_x = {}
         raw_w = {}
@@ -146,151 +74,310 @@ def tile_binarylinear_pa_kernel(tc, x, W1, g1, b1, W2, g2, b2, out):
 
         codes = {}
         scales = {}
-        for label in ("x", "w1", "h1", "w2"):
+        for label in ("x", "h1"):
             codes[label] = keep.tile([P, PASSES, SIZE], U32, name="codes_" + label, align_bytes=64)
             scales[label] = keep.tile([P, PASSES, SIZE], U8, name="scales_" + label, align_bytes=64)
+        w_codes = keep.tile([P, 2 * TILES, PASSES * P], U32, name="w_codes", align_bytes=64)
+        w_scales = keep.tile([P, 2 * TILES, PASSES * P], U8, name="w_scales", align_bytes=64)
 
-        signs = {}
+        x_banks = {}
+        x_grouped = {}
 
-        def take_signs(q):
-            signs[q] = sign_rows(nc, psum, stage, raw_w[q // 2][:, q % 2, :], ident)
+        def transpose_x(c):
+            for e in range(2):
+                x_banks[c, e] = psum.tile([P, BANK], F32, name="x_bank", tag="bank")
+                transpose_rows(nc, x_banks[c, e], raw_x[c][:, e, :], ident)
 
-        def quantise_signs(q):
-            label = "w1" if q < TILES else "w2"
-            quantise_columns(nc, signs[q], codes[label], scales[label], P * (q % TILES), P)
-
-        h1 = [keep.tile([P, 4, SIZE], BF16, name="h1_%d" % g) for g in range(PASSES)]
-        gains = keep.tile([P, 2 * TILES], F32, name="gains")
-        neg_gains = keep.tile([P, 2 * TILES], F32, name="neg_gains")
-        biases = keep.tile([P, 2 * TILES], F32, name="biases")
-        sums = {}
-        coeff = {}
-
-        def layer1_front(m):
-            sums[m] = mx_product(nc, psum, codes["w1"], scales["w1"], codes["x"], scales["x"], m)
-            coeff[m] = norm_coefficients(
-                nc, small, sums[m], gains[:, m : m + 1], neg_gains[:, m : m + 1], biases[:, m : m + 1], eps
+        def copy_x(c, e, copy):
+            if e == 0:
+                x_grouped[c] = stage.tile([P, PASSES * CHUNK * 4], BF16, name="grouped_x", bufs=2, align_bytes=64)
+            pairs = x_grouped[c][:].bitcast(F32).rearrange("p (g c u) -> p g c u", g=PASSES, u=2)
+            copy(
+                out=pairs[:, :, P * e : P * (e + 1), :],
+                in_=x_banks[c, e][:].rearrange("p (u g r) -> p g r u", g=PASSES, u=2),
             )
 
-        def layer1_normalise(m):
-            a, shift = coeff[m]
-            for half in range(HALVES):
-                nc.scalar.activation(
-                    out=h1[m // 4][:, m % 4, BANK * half : BANK * (half + 1)],
-                    in_=sums[m][half][:],
-                    func=ACT.Relu,
-                    bias=shift,
-                    scale=a,
-                )
-
-        def quantise_h1(g):
-            for half in range(HALVES):
-                cols = slice(BANK * half, BANK * (half + 1))
-                grouped = stage.tile([P, BANK * 4], BF16, tag="grouped_h", bufs=2, align_bytes=64)
-                nc.vector.tensor_copy(
-                    out=grouped[:].rearrange("p (c i t) -> p c t i", i=4, t=4),
-                    in_=h1[g][:, :, cols].rearrange("p t (c i) -> p c t i", i=4),
-                )
+        def quantise_x(c):
+            for g in range(PASSES):
+                cols = slice(CHUNK * c, CHUNK * (c + 1))
                 nc.vector.quantize_mx(
-                    out=codes["h1"][:, g, cols].bitcast(FP8X4),
-                    scales=scales["h1"][:, g, cols],
-                    in_=grouped[:],
+                    out=codes["x"][:, g, cols].bitcast(FP8X4),
+                    scales=scales["x"][:, g, cols],
+                    in_=x_grouped[c][:, 4 * CHUNK * g : 4 * CHUNK * (g + 1)],
                 )
 
-        take_signs(0)
-        take_signs(1)
-        for c in range(CHUNKS):
-            prepare_activations(nc, psum, stage, raw_x[c], ident, codes["x"], scales["x"], c)
-        quantise_signs(0)
-        quantise_signs(1)
+        w_rows = {}
+        w_banks = {}
+        w_grouped = {}
 
+        def clamp(q):
+            clamped = stage.tile([P, SIZE], BF16, tag="clamped", bufs=3)
+            nc.vector.tensor_scalar(
+                out=clamped[:], in0=raw_w[q // 2][:, q % 2, :], scalar1=-TINY, scalar2=TINY, op0=ALU.max, op1=ALU.min
+            )
+            w_rows[q] = clamped
+
+        def transpose_w(q):
+            w_banks[q] = psum.tile([P, BANK], F32, name="w_bank", tag="bank")
+            rows = w_rows[q][:] if q in w_rows else raw_w[q // 2][:, q % 2, :]
+            transpose_rows(nc, w_banks[q], rows, ident)
+
+        def take_signs(q):
+            w_grouped[q] = stage.tile([P, PASSES * P * 4], BF16, name="grouped_w", bufs=6, align_bytes=64)
+            src = w_banks[q][:].bitcast(BF16).rearrange("p (u gr e) -> p gr u e", u=2, e=2)
+            dst = w_grouped[q][:].rearrange("p (gr u e) -> p gr u e", u=2, e=2)
+            if q in w_rows:
+                nc.vector.tensor_scalar_mul(out=dst, in0=src, scalar1=1.0 / TINY)
+            else:
+                nc.scalar.activation(out=dst, in_=src, func=ACT.Sign)
+
+        def quantise_w(q):
+            nc.vector.quantize_mx(
+                out=w_codes[:, q, :].bitcast(FP8X4), scales=w_scales[:, q, :], in_=w_grouped[q][:]
+            )
+
+        sums = {}
+        stats = {}
+        mean_var = {}
+        rstd = {}
+        factors = {}
+        coeff = {}
+
+        def product(q, label, half):
+            cols = slice(BANK * half, BANK * (half + 1))
+            acc = psum.tile([P, BANK], F32, tag="bank")
+            sums[q, half] = acc
+            for g in range(PASSES):
+                nc.tensor.matmul_mx(
+                    out=acc[:],
+                    lhsT=w_codes[:, q, P * g : P * (g + 1)].bitcast(FP8X4),
+                    lhsT_scale=w_scales[:, q, P * g : P * (g + 1)],
+                    rhs=codes[label][:, g, cols].bitcast(FP8X4),
+                    rhs_scale=scales[label][:, g, cols],
+                    start=(g == 0),
+                    stop=(g == PASSES - 1),
+                )
+
+        def take_stats(q, half, values):
+            if half == 0:
+                stats[q] = small.tile([P, HALVES, 6], F32, name="stats")
+            nc.vector.bn_stats(out=stats[q][:, half, :], in_=values)
+
+        def aggregate(q):
+            mean_var[q] = small.tile([P, 2], F32, name="mean_var")
+            nc.vector.bn_aggr(out=mean_var[q][:], in_=stats[q][:].rearrange("p h s -> p (h s)"))
+
+        def take_rstd(q):
+            rstd[q] = small.tile([P, 1], F32, name="rstd")
+            nc.scalar.activation(out=rstd[q][:], in_=mean_var[q][:, 1:2], func=ACT.Abs_reciprocal_sqrt, bias=eps[:])
+
+        def take_factors(q):
+            factors[q] = small.tile([P, 2], F32, name="factors")
+            nc.vector.tensor_scalar_mul(out=factors[q][:], in0=gains[:, q, :], scalar1=rstd[q][:])
+
+        def take_shift(q):
+            coeff[q] = small.tile([P, 1], F32, name="shift")
+            nc.vector.tensor_scalar(
+                out=coeff[q][:],
+                in0=mean_var[q][:, 0:1],
+                scalar1=factors[q][:, 1:2],
+                scalar2=biases[:, q : q + 1],
+                op0=ALU.mult,
+                op1=ALU.add,
+            )
+
+        h1 = [keep.tile([P, 4, SIZE], BF16, name="h1_%d" % g) for g in range(PASSES)]
+        h_grouped = {}
+
+        def normalise_h(m, half):
+            nc.scalar.activation(
+                out=h1[m // 4][:, m % 4, BANK * half : BANK * (half + 1)],
+                in_=sums[m, half][:],
+                func=ACT.Relu,
+                bias=coeff[m][:],
+                scale=factors[m][:, 0:1],
+            )
+
+        def interleave_h(g, half, quarter, copy):
+            if quarter == 0:
+                h_grouped[g, half] = stage.tile([P, BANK * 4], BF16, name="grouped_h", bufs=2, align_bytes=64)
+            n = BANK // 2
+            src = slice(BANK * half + n * quarter, BANK * half + n * (quarter + 1))
+            dst = slice(4 * n * quarter, 4 * n * (quarter + 1))
+            copy(
+                out=h_grouped[g, half][:, dst].rearrange("p (c i t) -> p c t i", i=4, t=4),
+                in_=h1[g][:, :, src].rearrange("p t (c i) -> p c t i", i=4),
+            )
+
+        def quantise_h(g, half):
+            cols = slice(BANK * half, BANK * (half + 1))
+            nc.vector.quantize_mx(
+                out=codes["h1"][:, g, cols].bitcast(FP8X4),
+                scales=scales["h1"][:, g, cols],
+                in_=h_grouped[g, half][:],
+            )
+
+        transpose_w(0)
+        take_signs(0)
+        clamp(1)
+        transpose_w(1)
+        take_signs(1)
+        quantise_w(0)
+        for c in range(CHUNKS):
+            transpose_x(c)
+            copy_x(c, 0, nc.scalar.copy)
+            copy_x(c, 1, nc.vector.tensor_copy if c < 2 else nc.scalar.copy)
+            if c == 0:
+                quantise_w(1)
+            quantise_x(c)
         vector_bank = psum.tile([P, BANK], F32, tag="bank")
         nc.tensor.transpose(vector_bank[:, 0:P], vector_rows[:].bitcast(F32), ident[:])
-        nc.vector.tensor_copy(out=gains[:], in_=vector_bank[:, 0 : 2 * CHUNKS].bitcast(BF16))
-        nc.vector.tensor_scalar_mul(
-            out=neg_gains[:], in0=vector_bank[:, 0 : 2 * CHUNKS].bitcast(BF16), scalar1=-1.0
-        )
-        nc.vector.tensor_copy(out=biases[:], in_=vector_bank[:, 2 * CHUNKS : 4 * CHUNKS].bitcast(BF16))
+        gains = keep.tile([P, 2 * TILES, 2], F32, name="gains")
+        biases = keep.tile([P, 2 * TILES], F32, name="biases")
+        values = vector_bank[:, 0 : 4 * CHUNKS].bitcast(BF16)
+        nc.vector.tensor_copy(out=gains[:, :, 0], in_=values[:, 0 : 2 * TILES])
+        nc.vector.tensor_scalar_mul(out=gains[:, :, 1], in0=values[:, 0 : 2 * TILES], scalar1=-1.0)
+        nc.vector.tensor_copy(out=biases[:], in_=values[:, 2 * TILES : 4 * TILES])
+        transpose_w(2)
+        take_signs(2)
+        for half in range(HALVES):
+            product(0, "x", half)
+        transpose_w(3)
+        take_signs(3)
+        for half in range(HALVES):
+            product(1, "x", half)
+        transpose_w(4)
+        for half in range(HALVES):
+            take_stats(0, half, sums[0, half][:])
+        aggregate(0)
+        take_rstd(0)
+        quantise_w(2)
+        quantise_w(3)
+        take_factors(0)
+        take_shift(0)
 
-        for q in range(2, LEAD):
-            take_signs(q)
-            quantise_signs(q)
-        for m in range(AHEAD):
-            layer1_front(m)
+        on_scalar = [4, 5, 6, 7, 11, 12, 13, 14, 15]
+        on_vector = [None, None, 8, 9, 10]
+
+        def at(seq, n):
+            return seq[n : n + 1] if n < len(seq) and seq[n] is not None else []
 
         for m in range(TILES):
-            take_signs(LEAD + m)
-            quantise_signs(LEAD + m)
-            if m + AHEAD < TILES:
-                layer1_front(m + AHEAD)
-            layer1_normalise(m)
-            if m % 4 == 3:
-                quantise_h1(m // 4)
-        for q in range(LEAD + TILES, 2 * TILES):
-            take_signs(q)
-            quantise_signs(q)
+            for q in at(on_vector, m + 1):
+                clamp(q)
+            if m + 1 < TILES:
+                for half in range(HALVES):
+                    take_stats(m + 1, half, sums[m + 1, half][:])
+                aggregate(m + 1)
+            for half in range(HALVES):
+                normalise_h(m, half)
+            if m > 0:
+                for q in at(on_scalar, m - 1) + at(on_vector, m - 1):
+                    quantise_w(q)
+            for q in at(on_scalar, m + 1) + at(on_vector, m + 1):
+                transpose_w(q)
+            if m + 2 < TILES:
+                for half in range(HALVES):
+                    product(m + 2, "x", half)
+            if m + 1 < TILES:
+                take_rstd(m + 1)
+            for q in at(on_vector, m):
+                take_signs(q)
+            for q in at(on_scalar, m):
+                take_signs(q)
+            if m + 1 < TILES:
+                take_factors(m + 1)
+                take_shift(m + 1)
+            if m in (5, 6):
+                for quarter in range(2):
+                    interleave_h(0, m - 5, quarter, nc.vector.tensor_copy)
+                quantise_h(0, m - 5)
+        interleave_h(1, 0, 0, nc.vector.tensor_copy)
+        interleave_h(1, 0, 1, nc.vector.tensor_copy)
+        interleave_h(1, 1, 0, nc.scalar.copy)
+        quantise_h(1, 0)
+        take_signs(15)
+        interleave_h(1, 1, 1, nc.vector.tensor_copy)
+        quantise_h(1, 1)
 
         out_view = out.rearrange("(cb r eb) n -> cb r eb n", r=P, eb=2)
         relu = {}
         normed = {}
 
-        def layer2_product(m):
-            sums[m] = mx_product(nc, psum, codes["w2"], scales["w2"], codes["h1"], scales["h1"], m)
+        def relu_2(m, half):
+            if half == 0:
+                relu[m] = stage.tile([P, HALVES, BANK], F32, name="relu", bufs=4)
+            nc.scalar.activation(out=relu[m][:, half, :], in_=sums[TILES + m, half][:], func=ACT.Relu)
 
-        def layer2_relu(m):
-            relu[m] = stage.tile([P, HALVES, BANK], F32, name="relu", bufs=4)
-            for half in range(HALVES):
-                nc.scalar.activation(out=relu[m][:, half, :], in_=sums[m][half][:], func=ACT.Relu)
-            coeff[m] = norm_coefficients(
-                nc,
-                small,
-                [relu[m][:, half, :] for half in range(HALVES)],
-                gains[:, TILES + m : TILES + m + 1],
-                neg_gains[:, TILES + m : TILES + m + 1],
-                biases[:, TILES + m : TILES + m + 1],
-                eps,
-            )
-
-        def layer2_normalise(m):
-            a, shift = coeff[m]
-            normed[m] = stage.tile([P, SIZE], F32, name="normed", bufs=5)
-            nc.vector.tensor_scalar(
-                out=normed[m][:],
-                in0=relu[m][:].rearrange("p h b -> p (h b)"),
-                scalar1=a,
-                scalar2=shift,
+        def normalise_2(m, half, engine):
+            if half == 0:
+                normed[m] = stage.tile([P, SIZE], F32, name="normed", bufs=5)
+            engine.tensor_scalar(
+                out=normed[m][:, BANK * half : BANK * (half + 1)],
+                in0=relu[m][:, half, :],
+                scalar1=factors[TILES + m][:, 0:1],
+                scalar2=coeff[TILES + m][:],
                 op0=ALU.mult,
                 op1=ALU.add,
             )
 
-        def store_block(c, cb):
-            bank = psum.tile([P, BANK], F32, tag="bank")
+        blocks = {}
+
+        def transpose_block(c, cb):
+            blocks[c, cb] = psum.tile([P, BANK], F32, name="block", tag="bank")
             for eb in range(2):
                 for e in range(2):
                     w = 2 * eb + e
                     nc.tensor.transpose(
-                        bank[:, P * w : P * (w + 1)],
+                        blocks[c, cb][:, P * w : P * (w + 1)],
                         normed[2 * c + e][:, CHUNK * cb + P * eb : CHUNK * cb + P * (eb + 1)],
                         ident[:],
                     )
-            rows = stage.tile([P, 2, CHUNK], F32, tag="rows", bufs=4)
-            copy = nc.vector.tensor_copy if cb == CHUNKS - 1 else nc.scalar.copy
+
+        def store_block(c, cb, copy):
+            rows = stage.tile([P, 2, CHUNK], F32, tag="rows", bufs=8)
             copy(
                 out=rows[:].rearrange("p eb (j e) -> p eb j e", e=2),
-                in_=bank[:].rearrange("p (eb e j) -> p eb j e", eb=2, e=2),
+                in_=blocks[c, cb][:].rearrange("p (eb e j) -> p eb j e", eb=2, e=2),
             )
             nc.sync.dma_start(out=out_view[cb][:, :, CHUNK * c : CHUNK * (c + 1)], in_=rows[:])
 
-        layer2_product(0)
-        for i in range(TILES + STORE_LAG):
-            if NORM_LAG <= i < TILES + NORM_LAG:
-                layer2_normalise(i - NORM_LAG)
-            if i < TILES:
-                layer2_relu(i)
-            if i >= STORE_LAG:
-                c = (i - STORE_LAG) // 2
-                cb = 2 * ((i - STORE_LAG) % 2)
-                store_block(c, cb)
-                store_block(c, cb + 1)
-            if i + 1 < TILES:
-                layer2_product(i + 1)
+        LAG = 4
+        for half in range(HALVES):
+            for m in range(2):
+                product(TILES + m, "h1", half)
+        for i in range(TILES + LAG):
+            c, cb = (i - LAG) // 2, 2 * (i % 2)
+            if i >= LAG:
+                transpose_block(c, cb)
+                transpose_block(c, cb + 1)
+            if 2 <= i + 1 < TILES:
+                for half in range(HALVES):
+                    product(TILES + i + 1, "h1", half)
+            if 1 <= i < TILES + 1:
+                take_stats(TILES + i - 1, 0, relu[i - 1][:, 0, :])
+            if 2 <= i < TILES + 2:
+                take_factors(TILES + i - 2)
+                take_shift(TILES + i - 2)
+            if 1 <= i < TILES + 1:
+                take_stats(TILES + i - 1, 1, relu[i - 1][:, 1, :])
+                aggregate(TILES + i - 1)
+            if i == 0:
+                relu_2(0, 0)
+                relu_2(1, 0)
+                relu_2(0, 1)
+            elif i == 1:
+                relu_2(1, 1)
+            elif i < TILES:
+                relu_2(i, 0)
+                relu_2(i, 1)
+            if 2 <= i < TILES + 2:
+                for half in range(HALVES):
+                    normalise_2(i - 2, half, nc.vector if i == TILES + 1 and half == 0 else nc.gpsimd)
+            if 1 <= i < TILES + 1:
+                take_rstd(TILES + i - 1)
+            if i in (0, 1):
+                quantise_w(2 * TILES - 2 + i)
+            if i >= LAG:
+                store_block(c, cb, nc.scalar.copy)
+                store_block(c, cb + 1, nc.vector.tensor_copy)

@@ -90,7 +90,7 @@ def tile_binarylinear_pa_kernel(tc, x, W1, g1, b1, W2, g2, b2, out):
 
         def copy_x(c, e, copy):
             if e == 0:
-                x_grouped[c] = stage.tile([P, PASSES * CHUNK * 4], BF16, name="grouped_x", bufs=2, align_bytes=64)
+                x_grouped[c] = stage.tile([P, PASSES * CHUNK * 4], BF16, name="grouped_x", bufs=4, align_bytes=64)
             pairs = x_grouped[c][:].bitcast(F32).rearrange("p (g c u) -> p g c u", g=PASSES, u=2)
             copy(
                 out=pairs[:, :, P * e : P * (e + 1), :],
@@ -173,18 +173,30 @@ def tile_binarylinear_pa_kernel(tc, x, W1, g1, b1, W2, g2, b2, out):
 
         def take_factors(q):
             factors[q] = small.tile([P, 2], F32, name="factors")
-            nc.vector.tensor_scalar_mul(out=factors[q][:], in0=gains[:, q, :], scalar1=rstd[q][:])
+            if q < TILES:
+                nc.vector.tensor_scalar_mul(out=factors[q][:], in0=gains[:, q, :], scalar1=rstd[q][:])
+            else:
+                nc.scalar.activation(out=factors[q][:], in_=gains[:, q, :], func=ACT.Copy, scale=rstd[q][:])
 
         def take_shift(q):
             coeff[q] = small.tile([P, 1], F32, name="shift")
-            nc.vector.tensor_scalar(
-                out=coeff[q][:],
-                in0=mean_var[q][:, 0:1],
-                scalar1=factors[q][:, 1:2],
-                scalar2=biases[:, q : q + 1],
-                op0=ALU.mult,
-                op1=ALU.add,
-            )
+            if q < TILES:
+                nc.vector.tensor_scalar(
+                    out=coeff[q][:],
+                    in0=mean_var[q][:, 0:1],
+                    scalar1=factors[q][:, 1:2],
+                    scalar2=biases[:, q : q + 1],
+                    op0=ALU.mult,
+                    op1=ALU.add,
+                )
+            else:
+                nc.scalar.activation(
+                    out=coeff[q][:],
+                    in_=mean_var[q][:, 0:1],
+                    func=ACT.Identity,
+                    scale=factors[q][:, 1:2],
+                    bias=biases[:, q : q + 1],
+                )
 
         h1 = [keep.tile([P, 4, SIZE], BF16, name="h1_%d" % g) for g in range(PASSES)]
         h_grouped = {}
@@ -240,63 +252,76 @@ def tile_binarylinear_pa_kernel(tc, x, W1, g1, b1, W2, g2, b2, out):
         nc.vector.tensor_copy(out=biases[:], in_=values[:, 2 * TILES : 4 * TILES])
         transpose_w(2)
         take_signs(2)
-        for half in range(HALVES):
-            product(0, "x", half)
         transpose_w(3)
         take_signs(3)
         for half in range(HALVES):
-            product(1, "x", half)
-        transpose_w(4)
+            product(0, "x", half)
         for half in range(HALVES):
-            take_stats(0, half, sums[0, half][:])
+            product(1, "x", half)
+        take_stats(0, 0, sums[0, 0][:])
+        take_stats(0, 1, sums[0, 1][:])
+        quantise_w(2)
         aggregate(0)
         take_rstd(0)
-        quantise_w(2)
-        quantise_w(3)
+        transpose_w(4)
+        take_signs(4)
+        for half in range(HALVES):
+            product(2, "x", half)
+        take_stats(1, 0, sums[1, 0][:])
         take_factors(0)
+        take_stats(1, 1, sums[1, 1][:])
         take_shift(0)
-
-        on_scalar = [4, 5, 6, 7, 11, 12, 13, 14, 15]
-        on_vector = [None, None, 8, 9, 10]
-
-        def at(seq, n):
-            return seq[n : n + 1] if n < len(seq) and seq[n] is not None else []
+        quantise_w(3)
+        aggregate(1)
+        quantise_w(4)
+        scalar_plan = [[5], [6], [7], [8], [11], [], [], [12, 13]]
+        vector_plan = [[], [], [9], [10], [], [], [], []]
+        for q in scalar_plan[0]:
+            transpose_w(q)
 
         for m in range(TILES):
-            for q in at(on_vector, m + 1):
-                clamp(q)
-            if m + 1 < TILES:
-                for half in range(HALVES):
-                    take_stats(m + 1, half, sums[m + 1, half][:])
-                aggregate(m + 1)
-            for half in range(HALVES):
-                normalise_h(m, half)
-            if m > 0:
-                for q in at(on_scalar, m - 1) + at(on_vector, m - 1):
-                    quantise_w(q)
-            for q in at(on_scalar, m + 1) + at(on_vector, m + 1):
-                transpose_w(q)
-            if m + 2 < TILES:
-                for half in range(HALVES):
-                    product(m + 2, "x", half)
+            normalise_h(m, 0)
             if m + 1 < TILES:
                 take_rstd(m + 1)
-            for q in at(on_vector, m):
-                take_signs(q)
-            for q in at(on_scalar, m):
-                take_signs(q)
+            normalise_h(m, 1)
+            if m + 2 < TILES:
+                take_stats(m + 2, 0, sums[m + 2, 0][:])
+                take_stats(m + 2, 1, sums[m + 2, 1][:])
             if m + 1 < TILES:
                 take_factors(m + 1)
+            if m + 1 < TILES:
+                for q in vector_plan[m + 1]:
+                    clamp(q)
+            if m > 0:
+                for q in scalar_plan[m - 1] + vector_plan[m - 1]:
+                    quantise_w(q)
+            if m + 1 < TILES:
                 take_shift(m + 1)
+                for q in vector_plan[m]:
+                    take_signs(q)
+            if m + 2 < TILES:
+                aggregate(m + 2)
+            for q in scalar_plan[m]:
+                take_signs(q)
+            if m + 1 < TILES:
+                for q in scalar_plan[m + 1]:
+                    transpose_w(q)
+            if m + 3 < TILES:
+                for half in range(HALVES):
+                    product(m + 3, "x", half)
+            if m + 1 < TILES:
+                for q in vector_plan[m + 1]:
+                    transpose_w(q)
             if m in (5, 6):
                 for quarter in range(2):
                     interleave_h(0, m - 5, quarter, nc.vector.tensor_copy)
-                quantise_h(0, m - 5)
+            if m == 6:
+                quantise_h(0, 0)
+        quantise_h(0, 1)
         interleave_h(1, 0, 0, nc.vector.tensor_copy)
         interleave_h(1, 0, 1, nc.vector.tensor_copy)
         interleave_h(1, 1, 0, nc.scalar.copy)
         quantise_h(1, 0)
-        take_signs(15)
         interleave_h(1, 1, 1, nc.vector.tensor_copy)
         quantise_h(1, 1)
 
@@ -306,20 +331,20 @@ def tile_binarylinear_pa_kernel(tc, x, W1, g1, b1, W2, g2, b2, out):
 
         def relu_2(m, half):
             if half == 0:
-                relu[m] = stage.tile([P, HALVES, BANK], F32, name="relu", bufs=4)
+                relu[m] = stage.tile([P, HALVES, BANK], F32, name="relu", bufs=6)
             nc.scalar.activation(out=relu[m][:, half, :], in_=sums[TILES + m, half][:], func=ACT.Relu)
 
         def normalise_2(m, half, engine):
             if half == 0:
                 normed[m] = stage.tile([P, SIZE], F32, name="normed", bufs=5)
-            engine.tensor_scalar(
-                out=normed[m][:, BANK * half : BANK * (half + 1)],
-                in0=relu[m][:, half, :],
-                scalar1=factors[TILES + m][:, 0:1],
-                scalar2=coeff[TILES + m][:],
-                op0=ALU.mult,
-                op1=ALU.add,
-            )
+            values = normed[m][:, BANK * half : BANK * (half + 1)]
+            factor, shift = factors[TILES + m][:, 0:1], coeff[TILES + m][:]
+            if engine is nc.scalar:
+                nc.scalar.activation(out=values, in_=relu[m][:, half, :], func=ACT.Identity, scale=factor, bias=shift)
+            else:
+                engine.tensor_scalar(
+                    out=values, in0=relu[m][:, half, :], scalar1=factor, scalar2=shift, op0=ALU.mult, op1=ALU.add
+                )
 
         blocks = {}
 
@@ -342,42 +367,83 @@ def tile_binarylinear_pa_kernel(tc, x, W1, g1, b1, W2, g2, b2, out):
             )
             nc.sync.dma_start(out=out_view[cb][:, :, CHUNK * c : CHUNK * (c + 1)], in_=rows[:])
 
-        LAG = 4
+        def chain(m):
+            take_rstd(TILES + m)
+            take_factors(TILES + m)
+            take_shift(TILES + m)
+
+        def norm(m, engine):
+            for half in range(HALVES):
+                normalise_2(m, half, engine)
+
+        def two_blocks(c, cb):
+            transpose_block(c, cb)
+            transpose_block(c, cb + 1)
+
+        def store_two(c, cb):
+            store_block(c, cb, nc.scalar.copy)
+            store_block(c, cb + 1, nc.vector.tensor_copy)
+
         for half in range(HALVES):
             for m in range(2):
                 product(TILES + m, "h1", half)
-        for i in range(TILES + LAG):
-            c, cb = (i - LAG) // 2, 2 * (i % 2)
-            if i >= LAG:
-                transpose_block(c, cb)
-                transpose_block(c, cb + 1)
-            if 2 <= i + 1 < TILES:
+        LAST = TILES - 1
+        relu_2(0, 0)
+        relu_2(1, 0)
+        clamp(14)
+        take_stats(TILES, 0, relu[0][:, 0, :])
+        clamp(15)
+        relu_2(0, 1)
+        quantise_w(12)
+        quantise_w(13)
+        for i in range(1, TILES):
+            c, cb = (i - 5) // 2, 2 * ((i - 5) % 2)
+            if i + 1 < TILES:
                 for half in range(HALVES):
                     product(TILES + i + 1, "h1", half)
-            if 1 <= i < TILES + 1:
-                take_stats(TILES + i - 1, 0, relu[i - 1][:, 0, :])
-            if 2 <= i < TILES + 2:
-                take_factors(TILES + i - 2)
-                take_shift(TILES + i - 2)
-            if 1 <= i < TILES + 1:
-                take_stats(TILES + i - 1, 1, relu[i - 1][:, 1, :])
-                aggregate(TILES + i - 1)
-            if i == 0:
-                relu_2(0, 0)
-                relu_2(1, 0)
-                relu_2(0, 1)
-            elif i == 1:
-                relu_2(1, 1)
-            elif i < TILES:
+            if i in (1, 2):
+                transpose_w(13 + i)
+            if i >= 5:
+                two_blocks(c, cb)
+            if i > 1:
                 relu_2(i, 0)
-                relu_2(i, 1)
-            if 2 <= i < TILES + 2:
-                for half in range(HALVES):
-                    normalise_2(i - 2, half, nc.vector if i == TILES + 1 and half == 0 else nc.gpsimd)
-            if 1 <= i < TILES + 1:
-                take_rstd(TILES + i - 1)
-            if i in (0, 1):
-                quantise_w(2 * TILES - 2 + i)
-            if i >= LAG:
-                store_block(c, cb, nc.scalar.copy)
-                store_block(c, cb + 1, nc.vector.tensor_copy)
+            if i >= 2:
+                take_rstd(TILES + i - 2)
+            relu_2(i, 1)
+            if i >= 2:
+                take_factors(TILES + i - 2)
+            take_stats(TILES + i - 1, 1, relu[i - 1][:, 1, :])
+            take_stats(TILES + i, 0, relu[i][:, 0, :])
+            aggregate(TILES + i - 1)
+            if i in (1, 2):
+                take_signs(13 + i)
+            if i in (2, 3):
+                quantise_w(12 + i)
+            if i >= 5:
+                store_two(c, cb)
+            if i >= 2:
+                take_shift(TILES + i - 2)
+                norm(i - 2, nc.vector if i < 4 else nc.gpsimd)
+        take_rstd(TILES + LAST - 1)
+        take_factors(TILES + LAST - 1)
+        take_stats(TILES + LAST, 1, relu[LAST][:, 1, :])
+        two_blocks(1, 2)
+        store_block(1, 2, nc.scalar.copy)
+        take_shift(TILES + LAST - 1)
+        norm(LAST - 1, nc.gpsimd)
+        aggregate(TILES + LAST)
+        store_block(1, 3, nc.vector.tensor_copy)
+        chain(LAST)
+        two_blocks(2, 0)
+        store_block(2, 0, nc.vector.tensor_copy)
+        norm(LAST, nc.scalar)
+        two_blocks(2, 2)
+        store_block(2, 1, nc.vector.tensor_copy)
+        store_block(2, 2, nc.vector.tensor_copy)
+        store_block(2, 3, nc.scalar.copy)
+        two_blocks(3, 0)
+        two_blocks(3, 2)
+        store_block(3, 0, nc.vector.tensor_copy)
+        store_block(3, 1, nc.scalar.copy)
+        store_block(3, 2, nc.vector.tensor_copy)
+        store_block(3, 3, nc.scalar.copy)

@@ -21,7 +21,7 @@ TILES = SIZE // P
 BANK = 512
 HALVES = SIZE // BANK
 EPS = 1e-5
-TINY = 2.0**-126
+HUGE = 2.0**126
 FLOPS = 2 * 2 * SIZE * SIZE * SIZE
 
 
@@ -46,7 +46,6 @@ def tile_binarylinear_pa_kernel(tc, x, W1, g1, b1, W2, g2, b2, out):
         stage = ctx.enter_context(tc.tile_pool(name="stage", bufs=4))
         small = ctx.enter_context(tc.tile_pool(name="small", bufs=6))
         psum = ctx.enter_context(tc.psum_pool(name="psum", bufs=8))
-        ctx.enter_context(tc.manual_schedule())
 
         eps = keep.tile([P, 1], F32, name="eps")
         nc.vector.memset(eps[:], EPS)
@@ -54,6 +53,11 @@ def tile_binarylinear_pa_kernel(tc, x, W1, g1, b1, W2, g2, b2, out):
         nc.vector.memset(vector_rows[:], 0.0)
         ident = keep.tile([P, P], F32, name="ident")
         make_identity(nc, ident[:])
+        ones = keep.tile([P, P], BF16, name="ones")
+        make_identity(nc, ones[:])
+        magnifier = keep.tile([P, P], BF16, name="magnifier")
+        nc.vector.tensor_scalar_mul(out=magnifier[:], in0=ones[:], scalar1=HUGE)
+        magnified = (1, 8, 9, 10, 12, 13, 14, 15)
         for v, vec in enumerate((g1, g2, b1, b2)):
             nc.scalar.dma_start(
                 out=vector_rows[CHUNKS * v : CHUNKS * (v + 1), :],
@@ -106,29 +110,43 @@ def tile_binarylinear_pa_kernel(tc, x, W1, g1, b1, W2, g2, b2, out):
                     in_=x_grouped[c][:, 4 * CHUNK * g : 4 * CHUNK * (g + 1)],
                 )
 
-        w_rows = {}
         w_banks = {}
         w_grouped = {}
 
-        def clamp(q):
-            clamped = stage.tile([P, SIZE], BF16, tag="clamped", bufs=3)
-            nc.vector.tensor_scalar(
-                out=clamped[:], in0=raw_w[q // 2][:, q % 2, :], scalar1=-TINY, scalar2=TINY, op0=ALU.max, op1=ALU.min
-            )
-            w_rows[q] = clamped
-
         def transpose_w(q):
-            w_banks[q] = psum.tile([P, BANK], F32, name="w_bank", tag="bank")
-            rows = w_rows[q][:] if q in w_rows else raw_w[q // 2][:, q % 2, :]
-            transpose_rows(nc, w_banks[q], rows, ident)
+            rows = raw_w[q // 2][:, q % 2, :]
+            if q in magnified:
+                w_banks[q] = psum.tile([P, 2 * BANK], BF16, name="wide_bank", tag="bank")
+                for block in range(4):
+                    g, u = block % 2, block // 2
+                    first = K_PASS * g + CHUNK * u
+                    pairs = w_banks[q][:, CHUNK * block : CHUNK * (block + 1)].rearrange("p (r e) -> p r e", e=2)
+                    nc.tensor.matmul(
+                        pairs,
+                        lhsT=rows[:, first + 1 : first + CHUNK : 2],
+                        rhs=magnifier[:].unsqueeze(2).to_broadcast([P, P, 2]),
+                        start=True,
+                        stop=True,
+                    )
+                    nc.tensor.matmul(
+                        pairs[:, :, 0],
+                        lhsT=rows[:, first : first + CHUNK : 2],
+                        rhs=magnifier[:],
+                        start=True,
+                        stop=True,
+                    )
+            else:
+                w_banks[q] = psum.tile([P, BANK], F32, name="w_bank", tag="bank")
+                transpose_rows(nc, w_banks[q], rows, ident)
 
         def take_signs(q):
             w_grouped[q] = stage.tile([P, PASSES * P * 4], BF16, name="grouped_w", bufs=6, align_bytes=64)
-            src = w_banks[q][:].bitcast(BF16).rearrange("p (u gr e) -> p gr u e", u=2, e=2)
             dst = w_grouped[q][:].rearrange("p (gr u e) -> p gr u e", u=2, e=2)
-            if q in w_rows:
-                nc.vector.tensor_scalar_mul(out=dst, in0=src, scalar1=1.0 / TINY)
+            if q in magnified:
+                src = w_banks[q][:].rearrange("p (u gr e) -> p gr u e", u=2, e=2)
+                nc.vector.tensor_scalar(out=dst, in0=src, scalar1=-1.0, scalar2=1.0, op0=ALU.max, op1=ALU.min)
             else:
+                src = w_banks[q][:].bitcast(BF16).rearrange("p (u gr e) -> p gr u e", u=2, e=2)
                 nc.scalar.activation(out=dst, in_=src, func=ACT.Sign)
 
         def quantise_w(q):
@@ -173,30 +191,17 @@ def tile_binarylinear_pa_kernel(tc, x, W1, g1, b1, W2, g2, b2, out):
 
         def take_factors(q):
             factors[q] = small.tile([P, 2], F32, name="factors")
-            if q < TILES:
-                nc.vector.tensor_scalar_mul(out=factors[q][:], in0=gains[:, q, :], scalar1=rstd[q][:])
-            else:
-                nc.scalar.activation(out=factors[q][:], in_=gains[:, q, :], func=ACT.Copy, scale=rstd[q][:])
+            nc.scalar.activation(out=factors[q][:], in_=gains[:, q, :], func=ACT.Copy, scale=rstd[q][:])
 
         def take_shift(q):
             coeff[q] = small.tile([P, 1], F32, name="shift")
-            if q < TILES:
-                nc.vector.tensor_scalar(
-                    out=coeff[q][:],
-                    in0=mean_var[q][:, 0:1],
-                    scalar1=factors[q][:, 1:2],
-                    scalar2=biases[:, q : q + 1],
-                    op0=ALU.mult,
-                    op1=ALU.add,
-                )
-            else:
-                nc.scalar.activation(
-                    out=coeff[q][:],
-                    in_=mean_var[q][:, 0:1],
-                    func=ACT.Identity,
-                    scale=factors[q][:, 1:2],
-                    bias=biases[:, q : q + 1],
-                )
+            nc.scalar.activation(
+                out=coeff[q][:],
+                in_=mean_var[q][:, 0:1],
+                func=ACT.Identity,
+                scale=factors[q][:, 1:2],
+                bias=biases[:, q : q + 1],
+            )
 
         h1 = [keep.tile([P, 4, SIZE], BF16, name="h1_%d" % g) for g in range(PASSES)]
         h_grouped = {}
@@ -231,7 +236,6 @@ def tile_binarylinear_pa_kernel(tc, x, W1, g1, b1, W2, g2, b2, out):
 
         transpose_w(0)
         take_signs(0)
-        clamp(1)
         transpose_w(1)
         take_signs(1)
         quantise_w(0)
@@ -263,61 +267,54 @@ def tile_binarylinear_pa_kernel(tc, x, W1, g1, b1, W2, g2, b2, out):
         quantise_w(2)
         aggregate(0)
         take_rstd(0)
+        take_factors(0)
+        take_shift(0)
         transpose_w(4)
         take_signs(4)
         for half in range(HALVES):
             product(2, "x", half)
         take_stats(1, 0, sums[1, 0][:])
-        take_factors(0)
         take_stats(1, 1, sums[1, 1][:])
-        take_shift(0)
         quantise_w(3)
         aggregate(1)
         quantise_w(4)
-        scalar_plan = [[5], [6], [7], [8], [11], [], [], [12, 13]]
-        vector_plan = [[], [], [9], [10], [], [], [], []]
+        scalar_plan = [[5], [6], [7], [11], [], [], [], []]
+        vector_plan = [[], [], [8], [9], [10], [12], [13], []]
         for q in scalar_plan[0]:
             transpose_w(q)
 
         for m in range(TILES):
-            normalise_h(m, 0)
             if m + 1 < TILES:
                 take_rstd(m + 1)
+            normalise_h(m, 0)
+            if m + 1 < TILES:
+                take_factors(m + 1)
             normalise_h(m, 1)
+            if m + 1 < TILES:
+                take_shift(m + 1)
             if m + 2 < TILES:
                 take_stats(m + 2, 0, sums[m + 2, 0][:])
                 take_stats(m + 2, 1, sums[m + 2, 1][:])
-            if m + 1 < TILES:
-                take_factors(m + 1)
-            if m + 1 < TILES:
-                for q in vector_plan[m + 1]:
-                    clamp(q)
             if m > 0:
                 for q in scalar_plan[m - 1] + vector_plan[m - 1]:
                     quantise_w(q)
-            if m + 1 < TILES:
-                take_shift(m + 1)
-                for q in vector_plan[m]:
-                    take_signs(q)
+            for q in vector_plan[m]:
+                take_signs(q)
             if m + 2 < TILES:
                 aggregate(m + 2)
             for q in scalar_plan[m]:
                 take_signs(q)
-            if m + 1 < TILES:
-                for q in scalar_plan[m + 1]:
-                    transpose_w(q)
+            if m in (4, 5):
+                interleave_h(0, m - 4, 0, nc.vector.tensor_copy)
+                interleave_h(0, m - 4, 1, nc.scalar.copy)
             if m + 3 < TILES:
                 for half in range(HALVES):
                     product(m + 3, "x", half)
             if m + 1 < TILES:
-                for q in vector_plan[m + 1]:
+                for q in vector_plan[m + 1] + scalar_plan[m + 1]:
                     transpose_w(q)
             if m in (5, 6):
-                for quarter in range(2):
-                    interleave_h(0, m - 5, quarter, nc.vector.tensor_copy)
-            if m == 6:
-                quantise_h(0, 0)
-        quantise_h(0, 1)
+                quantise_h(0, m - 5)
         interleave_h(1, 0, 0, nc.vector.tensor_copy)
         interleave_h(1, 0, 1, nc.vector.tensor_copy)
         interleave_h(1, 1, 0, nc.scalar.copy)
@@ -390,12 +387,8 @@ def tile_binarylinear_pa_kernel(tc, x, W1, g1, b1, W2, g2, b2, out):
         LAST = TILES - 1
         relu_2(0, 0)
         relu_2(1, 0)
-        clamp(14)
         take_stats(TILES, 0, relu[0][:, 0, :])
-        clamp(15)
         relu_2(0, 1)
-        quantise_w(12)
-        quantise_w(13)
         for i in range(1, TILES):
             c, cb = (i - 5) // 2, 2 * ((i - 5) % 2)
             if i + 1 < TILES:
@@ -423,7 +416,7 @@ def tile_binarylinear_pa_kernel(tc, x, W1, g1, b1, W2, g2, b2, out):
                 store_two(c, cb)
             if i >= 2:
                 take_shift(TILES + i - 2)
-                norm(i - 2, nc.vector if i < 4 else nc.gpsimd)
+                norm(i - 2, nc.gpsimd)
         take_rstd(TILES + LAST - 1)
         take_factors(TILES + LAST - 1)
         take_stats(TILES + LAST, 1, relu[LAST][:, 1, :])

@@ -46,6 +46,7 @@ def tile_binarylinear_pa_kernel(tc, x, W1, g1, b1, W2, g2, b2, out):
         stage = ctx.enter_context(tc.tile_pool(name="stage", bufs=4))
         small = ctx.enter_context(tc.tile_pool(name="small", bufs=6))
         psum = ctx.enter_context(tc.psum_pool(name="psum", bufs=8))
+        ctx.enter_context(tc.manual_schedule())
 
         eps = keep.tile([P, 1], F32, name="eps")
         nc.vector.memset(eps[:], EPS)
@@ -57,7 +58,7 @@ def tile_binarylinear_pa_kernel(tc, x, W1, g1, b1, W2, g2, b2, out):
         make_identity(nc, ones[:])
         magnifier = keep.tile([P, P], BF16, name="magnifier")
         nc.vector.tensor_scalar_mul(out=magnifier[:], in0=ones[:], scalar1=HUGE)
-        magnified = (1, 8, 9, 10, 12, 13, 14, 15)
+        magnified = (1, 8, 9, 10, 12, 14, 15)
         for v, vec in enumerate((g1, g2, b1, b2)):
             nc.scalar.dma_start(
                 out=vector_rows[CHUNKS * v : CHUNKS * (v + 1), :],
@@ -189,19 +190,24 @@ def tile_binarylinear_pa_kernel(tc, x, W1, g1, b1, W2, g2, b2, out):
             rstd[q] = small.tile([P, 1], F32, name="rstd")
             nc.scalar.activation(out=rstd[q][:], in_=mean_var[q][:, 1:2], func=ACT.Abs_reciprocal_sqrt, bias=eps[:])
 
-        def take_factors(q):
+        def take_factors(q, engine):
             factors[q] = small.tile([P, 2], F32, name="factors")
-            nc.scalar.activation(out=factors[q][:], in_=gains[:, q, :], func=ACT.Copy, scale=rstd[q][:])
+            if engine is nc.scalar:
+                nc.scalar.activation(out=factors[q][:], in_=gains[:, q, :], func=ACT.Copy, scale=rstd[q][:])
+            else:
+                engine.tensor_scalar(
+                    out=factors[q][:], in0=gains[:, q, :], scalar1=rstd[q][:], scalar2=0.0, op0=ALU.mult, op1=ALU.add
+                )
 
-        def take_shift(q):
+        def take_shift(q, engine):
             coeff[q] = small.tile([P, 1], F32, name="shift")
-            nc.scalar.activation(
-                out=coeff[q][:],
-                in_=mean_var[q][:, 0:1],
-                func=ACT.Identity,
-                scale=factors[q][:, 1:2],
-                bias=biases[:, q : q + 1],
-            )
+            mean, factor, bias = mean_var[q][:, 0:1], factors[q][:, 1:2], biases[:, q : q + 1]
+            if engine is nc.scalar:
+                nc.scalar.activation(out=coeff[q][:], in_=mean, func=ACT.Identity, scale=factor, bias=bias)
+            else:
+                engine.tensor_scalar(
+                    out=coeff[q][:], in0=mean, scalar1=factor, scalar2=bias, op0=ALU.mult, op1=ALU.add
+                )
 
         h1 = [keep.tile([P, 4, SIZE], BF16, name="h1_%d" % g) for g in range(PASSES)]
         h_grouped = {}
@@ -267,8 +273,8 @@ def tile_binarylinear_pa_kernel(tc, x, W1, g1, b1, W2, g2, b2, out):
         quantise_w(2)
         aggregate(0)
         take_rstd(0)
-        take_factors(0)
-        take_shift(0)
+        take_factors(0, nc.gpsimd)
+        take_shift(0, nc.gpsimd)
         transpose_w(4)
         take_signs(4)
         for half in range(HALVES):
@@ -278,30 +284,32 @@ def tile_binarylinear_pa_kernel(tc, x, W1, g1, b1, W2, g2, b2, out):
         quantise_w(3)
         aggregate(1)
         quantise_w(4)
-        scalar_plan = [[5], [6], [7], [11], [], [], [], []]
-        vector_plan = [[], [], [8], [9], [10], [12], [13], []]
+        scalar_plan = [[5], [6], [7], [11], [], [], [], [13]]
+        vector_plan = [[], [], [8], [9], [10], [12], [], []]
         for q in scalar_plan[0]:
             transpose_w(q)
+
+        late = (14, 15)
 
         for m in range(TILES):
             if m + 1 < TILES:
                 take_rstd(m + 1)
             normalise_h(m, 0)
             if m + 1 < TILES:
-                take_factors(m + 1)
+                take_factors(m + 1, nc.gpsimd)
             normalise_h(m, 1)
             if m + 1 < TILES:
-                take_shift(m + 1)
+                take_shift(m + 1, nc.gpsimd)
             if m + 2 < TILES:
                 take_stats(m + 2, 0, sums[m + 2, 0][:])
                 take_stats(m + 2, 1, sums[m + 2, 1][:])
             if m > 0:
                 for q in scalar_plan[m - 1] + vector_plan[m - 1]:
                     quantise_w(q)
-            for q in vector_plan[m]:
-                take_signs(q)
             if m + 2 < TILES:
                 aggregate(m + 2)
+            for q in vector_plan[m]:
+                take_signs(q)
             for q in scalar_plan[m]:
                 take_signs(q)
             if m in (4, 5):
@@ -321,6 +329,9 @@ def tile_binarylinear_pa_kernel(tc, x, W1, g1, b1, W2, g2, b2, out):
         quantise_h(1, 0)
         interleave_h(1, 1, 1, nc.vector.tensor_copy)
         quantise_h(1, 1)
+        for q in late:
+            transpose_w(q)
+        take_signs(late[0])
 
         out_view = out.rearrange("(cb r eb) n -> cb r eb n", r=P, eb=2)
         relu = {}
@@ -366,8 +377,8 @@ def tile_binarylinear_pa_kernel(tc, x, W1, g1, b1, W2, g2, b2, out):
 
         def chain(m):
             take_rstd(TILES + m)
-            take_factors(TILES + m)
-            take_shift(TILES + m)
+            take_factors(TILES + m, nc.scalar)
+            take_shift(TILES + m, nc.scalar)
 
         def norm(m, engine):
             for half in range(HALVES):
@@ -385,17 +396,17 @@ def tile_binarylinear_pa_kernel(tc, x, W1, g1, b1, W2, g2, b2, out):
             for m in range(2):
                 product(TILES + m, "h1", half)
         LAST = TILES - 1
+        unquantised = scalar_plan[-1] + vector_plan[-1] + list(late)
         relu_2(0, 0)
         relu_2(1, 0)
         take_stats(TILES, 0, relu[0][:, 0, :])
+        take_signs(late[1])
         relu_2(0, 1)
         for i in range(1, TILES):
             c, cb = (i - 5) // 2, 2 * ((i - 5) % 2)
             if i + 1 < TILES:
                 for half in range(HALVES):
                     product(TILES + i + 1, "h1", half)
-            if i in (1, 2):
-                transpose_w(13 + i)
             if i >= 5:
                 two_blocks(c, cb)
             if i > 1:
@@ -404,25 +415,23 @@ def tile_binarylinear_pa_kernel(tc, x, W1, g1, b1, W2, g2, b2, out):
                 take_rstd(TILES + i - 2)
             relu_2(i, 1)
             if i >= 2:
-                take_factors(TILES + i - 2)
+                take_factors(TILES + i - 2, nc.scalar)
             take_stats(TILES + i - 1, 1, relu[i - 1][:, 1, :])
             take_stats(TILES + i, 0, relu[i][:, 0, :])
             aggregate(TILES + i - 1)
-            if i in (1, 2):
-                take_signs(13 + i)
-            if i in (2, 3):
-                quantise_w(12 + i)
+            if i <= len(unquantised):
+                quantise_w(unquantised[i - 1])
             if i >= 5:
                 store_two(c, cb)
             if i >= 2:
-                take_shift(TILES + i - 2)
+                take_shift(TILES + i - 2, nc.scalar)
                 norm(i - 2, nc.gpsimd)
         take_rstd(TILES + LAST - 1)
-        take_factors(TILES + LAST - 1)
+        take_factors(TILES + LAST - 1, nc.scalar)
         take_stats(TILES + LAST, 1, relu[LAST][:, 1, :])
         two_blocks(1, 2)
         store_block(1, 2, nc.scalar.copy)
-        take_shift(TILES + LAST - 1)
+        take_shift(TILES + LAST - 1, nc.scalar)
         norm(LAST - 1, nc.gpsimd)
         aggregate(TILES + LAST)
         store_block(1, 3, nc.vector.tensor_copy)

@@ -58,7 +58,7 @@ def tile_binarylinear_pa_kernel(tc, x, W1, g1, b1, W2, g2, b2, out):
         make_identity(nc, ones[:])
         magnifier = keep.tile([P, P], BF16, name="magnifier")
         nc.vector.tensor_scalar_mul(out=magnifier[:], in0=ones[:], scalar1=HUGE)
-        magnified = (1, 8, 9, 10, 12, 14, 15)
+        magnified = (1, 7, 8, 9, 10, 12, 14, 15)
         for v, vec in enumerate((g1, g2, b1, b2)):
             nc.scalar.dma_start(
                 out=vector_rows[CHUNKS * v : CHUNKS * (v + 1), :],
@@ -162,20 +162,23 @@ def tile_binarylinear_pa_kernel(tc, x, W1, g1, b1, W2, g2, b2, out):
         factors = {}
         coeff = {}
 
-        def product(q, label, half):
+        def product_pass(q, label, half, g):
             cols = slice(BANK * half, BANK * (half + 1))
-            acc = psum.tile([P, BANK], F32, tag="bank")
-            sums[q, half] = acc
+            if g == 0:
+                sums[q, half] = psum.tile([P, BANK], F32, name="sum_bank", tag="bank")
+            nc.tensor.matmul_mx(
+                out=sums[q, half][:],
+                lhsT=w_codes[:, q, P * g : P * (g + 1)].bitcast(FP8X4),
+                lhsT_scale=w_scales[:, q, P * g : P * (g + 1)],
+                rhs=codes[label][:, g, cols].bitcast(FP8X4),
+                rhs_scale=scales[label][:, g, cols],
+                start=(g == 0),
+                stop=(g == PASSES - 1),
+            )
+
+        def product(q, label, half):
             for g in range(PASSES):
-                nc.tensor.matmul_mx(
-                    out=acc[:],
-                    lhsT=w_codes[:, q, P * g : P * (g + 1)].bitcast(FP8X4),
-                    lhsT_scale=w_scales[:, q, P * g : P * (g + 1)],
-                    rhs=codes[label][:, g, cols].bitcast(FP8X4),
-                    rhs_scale=scales[label][:, g, cols],
-                    start=(g == 0),
-                    stop=(g == PASSES - 1),
-                )
+                product_pass(q, label, half, g)
 
         def take_stats(q, half, values):
             if half == 0:
@@ -273,8 +276,8 @@ def tile_binarylinear_pa_kernel(tc, x, W1, g1, b1, W2, g2, b2, out):
         quantise_w(2)
         aggregate(0)
         take_rstd(0)
-        take_factors(0, nc.gpsimd)
-        take_shift(0, nc.gpsimd)
+        take_factors(0, nc.scalar)
+        take_shift(0, nc.scalar)
         transpose_w(4)
         take_signs(4)
         for half in range(HALVES):
@@ -284,8 +287,8 @@ def tile_binarylinear_pa_kernel(tc, x, W1, g1, b1, W2, g2, b2, out):
         quantise_w(3)
         aggregate(1)
         quantise_w(4)
-        scalar_plan = [[5], [6], [7], [11], [], [], [], [13]]
-        vector_plan = [[], [], [8], [9], [10], [12], [], []]
+        scalar_plan = [[5], [6], [], [11], [], [], [], [13]]
+        vector_plan = [[], [], [7], [8], [9], [10], [12], []]
         for q in scalar_plan[0]:
             transpose_w(q)
 
@@ -296,10 +299,10 @@ def tile_binarylinear_pa_kernel(tc, x, W1, g1, b1, W2, g2, b2, out):
                 take_rstd(m + 1)
             normalise_h(m, 0)
             if m + 1 < TILES:
-                take_factors(m + 1, nc.gpsimd)
+                take_factors(m + 1, nc.scalar)
             normalise_h(m, 1)
             if m + 1 < TILES:
-                take_shift(m + 1, nc.gpsimd)
+                take_shift(m + 1, nc.scalar)
             if m + 2 < TILES:
                 take_stats(m + 2, 0, sums[m + 2, 0][:])
                 take_stats(m + 2, 1, sums[m + 2, 1][:])
@@ -392,9 +395,10 @@ def tile_binarylinear_pa_kernel(tc, x, W1, g1, b1, W2, g2, b2, out):
             store_block(c, cb, nc.scalar.copy)
             store_block(c, cb + 1, nc.vector.tensor_copy)
 
-        for half in range(HALVES):
-            for m in range(2):
-                product(TILES + m, "h1", half)
+        for g in range(PASSES):
+            for half in range(HALVES):
+                for m in range(2):
+                    product_pass(TILES + m, "h1", half, g)
         LAST = TILES - 1
         unquantised = scalar_plan[-1] + vector_plan[-1] + list(late)
         relu_2(0, 0)

@@ -224,16 +224,19 @@ def tile_binarylinear_pa_kernel(tc, x, W1, g1, b1, W2, g2, b2, out):
                 scale=factors[m][:, 0:1],
             )
 
-        def interleave_h(g, half, quarter, copy):
-            if quarter == 0:
+        def interleave_h(g, half, part, parts, copy):
+            if part == 0:
                 h_grouped[g, half] = stage.tile([P, BANK * 4], BF16, name="grouped_h", bufs=2, align_bytes=64)
-            n = BANK // 2
-            src = slice(BANK * half + n * quarter, BANK * half + n * (quarter + 1))
-            dst = slice(4 * n * quarter, 4 * n * (quarter + 1))
+            n = BANK // parts
+            src = slice(BANK * half + n * part, BANK * half + n * (part + 1))
+            dst = slice(4 * n * part, 4 * n * (part + 1))
             copy(
                 out=h_grouped[g, half][:, dst].rearrange("p (c i t) -> p c t i", i=4, t=4),
                 in_=h1[g][:, :, src].rearrange("p t (c i) -> p c t i", i=4),
             )
+
+        def gpsimd_copy(out, in_):
+            nc.gpsimd.tensor_scalar(out=out, in0=in_, scalar1=1.0, scalar2=0.0, op0=ALU.mult, op1=ALU.add)
 
         def quantise_h(g, half):
             cols = slice(BANK * half, BANK * (half + 1))
@@ -269,6 +272,8 @@ def tile_binarylinear_pa_kernel(tc, x, W1, g1, b1, W2, g2, b2, out):
         take_signs(3)
         for half in range(HALVES):
             product(0, "x", half)
+        transpose_w(4)
+        take_signs(4)
         for half in range(HALVES):
             product(1, "x", half)
         take_stats(0, 0, sums[0, 0][:])
@@ -278,8 +283,6 @@ def tile_binarylinear_pa_kernel(tc, x, W1, g1, b1, W2, g2, b2, out):
         take_rstd(0)
         take_factors(0, nc.scalar)
         take_shift(0, nc.scalar)
-        transpose_w(4)
-        take_signs(4)
         for half in range(HALVES):
             product(2, "x", half)
         take_stats(1, 0, sums[1, 0][:])
@@ -289,15 +292,18 @@ def tile_binarylinear_pa_kernel(tc, x, W1, g1, b1, W2, g2, b2, out):
         quantise_w(4)
         scalar_plan = [[5], [6], [], [11], [], [], [], [13]]
         vector_plan = [[], [], [7], [8], [9], [10], [12], []]
-        for q in scalar_plan[0]:
+        for q in scalar_plan[0] + vector_plan[0]:
             transpose_w(q)
 
         late = (14, 15)
 
         for m in range(TILES):
+            if m == 0:
+                normalise_h(m, 0)
             if m + 1 < TILES:
                 take_rstd(m + 1)
-            normalise_h(m, 0)
+            if m > 0:
+                normalise_h(m, 0)
             if m + 1 < TILES:
                 take_factors(m + 1, nc.scalar)
             normalise_h(m, 1)
@@ -316,8 +322,8 @@ def tile_binarylinear_pa_kernel(tc, x, W1, g1, b1, W2, g2, b2, out):
             for q in scalar_plan[m]:
                 take_signs(q)
             if m in (4, 5):
-                interleave_h(0, m - 4, 0, nc.vector.tensor_copy)
-                interleave_h(0, m - 4, 1, nc.scalar.copy)
+                for part in range(4):
+                    interleave_h(0, m - 4, part, 4, gpsimd_copy)
             if m + 3 < TILES:
                 for half in range(HALVES):
                     product(m + 3, "x", half)
@@ -326,11 +332,11 @@ def tile_binarylinear_pa_kernel(tc, x, W1, g1, b1, W2, g2, b2, out):
                     transpose_w(q)
             if m in (5, 6):
                 quantise_h(0, m - 5)
-        interleave_h(1, 0, 0, nc.vector.tensor_copy)
-        interleave_h(1, 0, 1, nc.vector.tensor_copy)
-        interleave_h(1, 1, 0, nc.scalar.copy)
+        interleave_h(1, 0, 0, 2, nc.vector.tensor_copy)
+        interleave_h(1, 0, 1, 2, nc.vector.tensor_copy)
+        interleave_h(1, 1, 0, 2, nc.scalar.copy)
         quantise_h(1, 0)
-        interleave_h(1, 1, 1, nc.vector.tensor_copy)
+        interleave_h(1, 1, 1, 2, nc.vector.tensor_copy)
         quantise_h(1, 1)
         for q in late:
             transpose_w(q)

from contextlib import ExitStack

import concourse.mybir as mybir
from concourse.masks import make_identity

F32 = mybir.dt.float32
BF16 = mybir.dt.bfloat16
U32 = mybir.dt.uint32
U8 = mybir.dt.uint8
FP8X4 = mybir.dt.float8_e4m3fn_x4
ACT = mybir.ActivationFunctionType
ALU = mybir.AluOpType

P = 128
SIZE = 1024
K_PASS = 512
PASSES = SIZE // K_PASS
CHUNK = 2 * P
CHUNKS = SIZE // CHUNK
TILES = SIZE // P
BANK = 512
HALVES = SIZE // BANK
EPS = 1e-5
HUGE = 2.0**126
FLOPS = 2 * 2 * SIZE * SIZE * SIZE


def load_chunk(nc, pool, src, label, c):
    raw = pool.tile([P, 2, SIZE], BF16, name="raw_%s%d" % (label, c))
    nc.sync.dma_start(out=raw[:], in_=src.rearrange("(c r e) k -> c r e k", r=P, e=2)[c])
    return raw


def transpose_rows(nc, bank, rows, ident):
    words = rows.bitcast(F32)
    for w in range(BANK // P):
        g, u = w // 2, w % 2
        block = PASSES * u + g
        nc.tensor.transpose(bank[:, P * block : P * (block + 1)], words[:, P * w : P * (w + 1)], ident[:])


def tile_binarylinear_pa_kernel(tc, x, W1, g1, b1, W2, g2, b2, out):
    nc = tc.nc
    with ExitStack() as ctx:
        keep = ctx.enter_context(tc.tile_pool(name="keep", bufs=1))
        stage = ctx.enter_context(tc.tile_pool(name="stage", bufs=4))
        small = ctx.enter_context(tc.tile_pool(name="small", bufs=6))
        psum = ctx.enter_context(tc.psum_pool(name="psum", bufs=8))
        ctx.enter_context(tc.manual_schedule())

        eps = keep.tile([P, 1], F32, name="eps")
        nc.vector.memset(eps[:], EPS)
        vector_rows = keep.tile([P, CHUNK], BF16, name="vector_rows")
        nc.vector.memset(vector_rows[:], 0.0)
        ident = keep.tile([P, P], F32, name="ident")
        make_identity(nc, ident[:])
        ones = keep.tile([P, P], BF16, name="ones")
        make_identity(nc, ones[:])
        magnifier = keep.tile([P, P], BF16, name="magnifier")
        nc.vector.tensor_scalar_mul(out=magnifier[:], in0=ones[:], scalar1=HUGE)
        magnified = (1, 7, 8, 9, 10, 12, 14, 15)
        for v, vec in enumerate((g1, g2, b1, b2)):
            nc.scalar.dma_start(
                out=vector_rows[CHUNKS * v : CHUNKS * (v + 1), :],
                in_=vec.rearrange("(c n) -> c n", n=CHUNK),
            )
        warm = keep.tile([P, 1], F32, name="warm")
        nc.scalar.activation(out=warm[:], in_=eps[:], func=ACT.Abs_reciprocal_sqrt)

        raw_x = {}
        raw_w = {}
        raw_w[0] = load_chunk(nc, keep, W1, "w", 0)
        for c in range(CHUNKS):
            raw_x[c] = load_chunk(nc, keep, x, "x", c)
        for c in range(1, CHUNKS):
            raw_w[c] = load_chunk(nc, keep, W1, "w", c)
        for c in range(CHUNKS):
            raw_w[CHUNKS + c] = load_chunk(nc, keep, W2, "v", c)

        codes = {}
        scales = {}
        for label in ("x", "h1"):
            codes[label] = keep.tile([P, PASSES, SIZE], U32, name="codes_" + label, align_bytes=64)
            scales[label] = keep.tile([P, PASSES, SIZE], U8, name="scales_" + label, align_bytes=64)
        w_codes = keep.tile([P, 2 * TILES, PASSES * P], U32, name="w_codes", align_bytes=64)
        w_scales = keep.tile([P, 2 * TILES, PASSES * P], U8, name="w_scales", align_bytes=64)

        x_banks = {}
        x_grouped = {}

        def transpose_x(c):
            for e in range(2):
                x_banks[c, e] = psum.tile([P, BANK], F32, name="x_bank", tag="bank")
                transpose_rows(nc, x_banks[c, e], raw_x[c][:, e, :], ident)

        def copy_x(c, e, copy):
            if e == 0:
                x_grouped[c] = stage.tile([P, PASSES * CHUNK * 4], BF16, name="grouped_x", bufs=4, align_bytes=64)
            pairs = x_grouped[c][:].bitcast(F32).rearrange("p (g c u) -> p g c u", g=PASSES, u=2)
            copy(
                out=pairs[:, :, P * e : P * (e + 1), :],
                in_=x_banks[c, e][:].rearrange("p (u g r) -> p g r u", g=PASSES, u=2),
            )

        def quantise_x(c):
            for g in range(PASSES):
                cols = slice(CHUNK * c, CHUNK * (c + 1))
                nc.vector.quantize_mx(
                    out=codes["x"][:, g, cols].bitcast(FP8X4),
                    scales=scales["x"][:, g, cols],
                    in_=x_grouped[c][:, 4 * CHUNK * g : 4 * CHUNK * (g + 1)],
                )

        w_banks = {}
        w_grouped = {}

        def transpose_w(q):
            rows = raw_w[q // 2][:, q % 2, :]
            if q in magnified:
                w_banks[q] = psum.tile([P, 2 * BANK], BF16, name="wide_bank", tag="bank")
                for block in range(4):
                    g, u = block % 2, block // 2
                    first = K_PASS * g + CHUNK * u
                    pairs = w_banks[q][:, CHUNK * block : CHUNK * (block + 1)].rearrange("p (r e) -> p r e", e=2)
                    nc.tensor.matmul(
                        pairs,
                        lhsT=rows[:, first + 1 : first + CHUNK : 2],
                        rhs=magnifier[:].unsqueeze(2).to_broadcast([P, P, 2]),
                        start=True,
                        stop=True,
                    )
                    nc.tensor.matmul(
                        pairs[:, :, 0],
                        lhsT=rows[:, first : first + CHUNK : 2],
                        rhs=magnifier[:],
                        start=True,
                        stop=True,
                    )
            else:
                w_banks[q] = psum.tile([P, BANK], F32, name="w_bank", tag="bank")
                transpose_rows(nc, w_banks[q], rows, ident)

        def take_signs(q):
            w_grouped[q] = stage.tile([P, PASSES * P * 4], BF16, name="grouped_w", bufs=6, align_bytes=64)
            dst = w_grouped[q][:].rearrange("p (gr u e) -> p gr u e", u=2, e=2)
            if q in magnified:
                src = w_banks[q][:].rearrange("p (u gr e) -> p gr u e", u=2, e=2)
                nc.vector.tensor_scalar(out=dst, in0=src, scalar1=-1.0, scalar2=1.0, op0=ALU.max, op1=ALU.min)
            else:
                src = w_banks[q][:].bitcast(BF16).rearrange("p (u gr e) -> p gr u e", u=2, e=2)
                nc.scalar.activation(out=dst, in_=src, func=ACT.Sign)

        def quantise_w(q):
            nc.vector.quantize_mx(
                out=w_codes[:, q, :].bitcast(FP8X4), scales=w_scales[:, q, :], in_=w_grouped[q][:]
            )

        sums = {}
        stats = {}
        mean_var = {}
        rstd = {}
        factors = {}
        coeff = {}

        def product_pass(q, label, half, g):
            cols = slice(BANK * half, BANK * (half + 1))
            if g == 0:
                sums[q, half] = psum.tile([P, BANK], F32, name="sum_bank", tag="bank")
            nc.tensor.matmul_mx(
                out=sums[q, half][:],
                lhsT=w_codes[:, q, P * g : P * (g + 1)].bitcast(FP8X4),
                lhsT_scale=w_scales[:, q, P * g : P * (g + 1)],
                rhs=codes[label][:, g, cols].bitcast(FP8X4),
                rhs_scale=scales[label][:, g, cols],
                start=(g == 0),
                stop=(g == PASSES - 1),
            )

        def product(q, label, half):
            for g in range(PASSES):
                product_pass(q, label, half, g)

        def take_stats(q, half, values):
            if half == 0:
                stats[q] = small.tile([P, HALVES, 6], F32, name="stats")
            nc.vector.bn_stats(out=stats[q][:, half, :], in_=values)

        def aggregate(q):
            mean_var[q] = small.tile([P, 2], F32, name="mean_var")
            nc.vector.bn_aggr(out=mean_var[q][:], in_=stats[q][:].rearrange("p h s -> p (h s)"))

        def take_rstd(q):
            rstd[q] = small.tile([P, 1], F32, name="rstd")
            nc.scalar.activation(out=rstd[q][:], in_=mean_var[q][:, 1:2], func=ACT.Abs_reciprocal_sqrt, bias=eps[:])

        def take_factors(q, engine):
            factors[q] = small.tile([P, 2], F32, name="factors")
            if engine is nc.scalar:
                nc.scalar.activation(out=factors[q][:], in_=gains[:, q, :], func=ACT.Copy, scale=rstd[q][:])
            else:
                engine.tensor_scalar(
                    out=factors[q][:], in0=gains[:, q, :], scalar1=rstd[q][:], scalar2=0.0, op0=ALU.mult, op1=ALU.add
                )

        def take_shift(q, engine):
            coeff[q] = small.tile([P, 1], F32, name="shift")
            mean, factor, bias = mean_var[q][:, 0:1], factors[q][:, 1:2], biases[:, q : q + 1]
            if engine is nc.scalar:
                nc.scalar.activation(out=coeff[q][:], in_=mean, func=ACT.Identity, scale=factor, bias=bias)
            else:
                engine.tensor_scalar(
                    out=coeff[q][:], in0=mean, scalar1=factor, scalar2=bias, op0=ALU.mult, op1=ALU.add
                )

        h1 = [keep.tile([P, 4, SIZE], BF16, name="h1_%d" % g) for g in range(PASSES)]
        h_grouped = {}

        def normalise_h(m, half):
            nc.scalar.activation(
                out=h1[m // 4][:, m % 4, BANK * half : BANK * (half + 1)],
                in_=sums[m, half][:],
                func=ACT.Relu,
                bias=coeff[m][:],
                scale=factors[m][:, 0:1],
            )

        def interleave_h(g, half, part, parts, copy):
            if part == 0:
                h_grouped[g, half] = stage.tile([P, BANK * 4], BF16, name="grouped_h", bufs=2, align_bytes=64)
            n = BANK // parts
            src = slice(BANK * half + n * part, BANK * half + n * (part + 1))
            dst = slice(4 * n * part, 4 * n * (part + 1))
            copy(
                out=h_grouped[g, half][:, dst].rearrange("p (c i t) -> p c t i", i=4, t=4),
                in_=h1[g][:, :, src].rearrange("p t (c i) -> p c t i", i=4),
            )

        def gpsimd_copy(out, in_):
            nc.gpsimd.tensor_scalar(out=out, in0=in_, scalar1=1.0, scalar2=0.0, op0=ALU.mult, op1=ALU.add)

        def quantise_h(g, half):
            cols = slice(BANK * half, BANK * (half + 1))
            nc.vector.quantize_mx(
                out=codes["h1"][:, g, cols].bitcast(FP8X4),
                scales=scales["h1"][:, g, cols],
                in_=h_grouped[g, half][:],
            )

        transpose_w(0)
        take_signs(0)
        transpose_w(1)
        take_signs(1)
        quantise_w(0)
        for c in range(CHUNKS):
            transpose_x(c)
            copy_x(c, 0, nc.scalar.copy)
            copy_x(c, 1, nc.vector.tensor_copy if c < 2 else nc.scalar.copy)
            if c == 0:
                quantise_w(1)
            quantise_x(c)
        vector_bank = psum.tile([P, BANK], F32, tag="bank")
        nc.tensor.transpose(vector_bank[:, 0:P], vector_rows[:].bitcast(F32), ident[:])
        gains = keep.tile([P, 2 * TILES, 2], F32, name="gains")
        biases = keep.tile([P, 2 * TILES], F32, name="biases")
        values = vector_bank[:, 0 : 4 * CHUNKS].bitcast(BF16)
        nc.vector.tensor_copy(out=gains[:, :, 0], in_=values[:, 0 : 2 * TILES])
        nc.vector.tensor_scalar_mul(out=gains[:, :, 1], in0=values[:, 0 : 2 * TILES], scalar1=-1.0)
        nc.vector.tensor_copy(out=biases[:], in_=values[:, 2 * TILES : 4 * TILES])
        transpose_w(2)
        take_signs(2)
        transpose_w(3)
        take_signs(3)
        for half in range(HALVES):
            product(0, "x", half)
        transpose_w(4)
        take_signs(4)
        for half in range(HALVES):
            product(1, "x", half)
        take_stats(0, 0, sums[0, 0][:])
        take_stats(0, 1, sums[0, 1][:])
        quantise_w(2)
        aggregate(0)
        take_rstd(0)
        take_factors(0, nc.scalar)
        take_shift(0, nc.scalar)
        for half in range(HALVES):
            product(2, "x", half)
        take_stats(1, 0, sums[1, 0][:])
        take_stats(1, 1, sums[1, 1][:])
        quantise_w(3)
        aggregate(1)
        quantise_w(4)
        scalar_plan = [[5], [6], [], [11], [], [], [], [13]]
        vector_plan = [[], [], [7], [8], [9], [10], [12], []]
        for q in scalar_plan[0] + vector_plan[0]:
            transpose_w(q)

        late = (14, 15)

        for m in range(TILES):
            if m == 0:
                normalise_h(m, 0)
            if m + 1 < TILES:
                take_rstd(m + 1)
            if m > 0:
                normalise_h(m, 0)
            if m + 1 < TILES:
                take_factors(m + 1, nc.scalar)
            normalise_h(m, 1)
            if m + 1 < TILES:
                take_shift(m + 1, nc.scalar)
            if m + 2 < TILES:
                take_stats(m + 2, 0, sums[m + 2, 0][:])
                take_stats(m + 2, 1, sums[m + 2, 1][:])
            if m > 0:
                for q in scalar_plan[m - 1] + vector_plan[m - 1]:
                    quantise_w(q)
            if m + 2 < TILES:
                aggregate(m + 2)
            for q in vector_plan[m]:
                take_signs(q)
            for q in scalar_plan[m]:
                take_signs(q)
            if m in (4, 5):
                for part in range(4):
                    interleave_h(0, m - 4, part, 4, gpsimd_copy)
            if m + 3 < TILES:
                for half in range(HALVES):
                    product(m + 3, "x", half)
            if m + 1 < TILES:
                for q in vector_plan[m + 1] + scalar_plan[m + 1]:
                    transpose_w(q)
            if m in (5, 6):
                quantise_h(0, m - 5)
        interleave_h(1, 0, 0, 2, nc.vector.tensor_copy)
        interleave_h(1, 0, 1, 2, nc.vector.tensor_copy)
        interleave_h(1, 1, 0, 2, nc.scalar.copy)
        quantise_h(1, 0)
        interleave_h(1, 1, 1, 2, nc.vector.tensor_copy)
        quantise_h(1, 1)
        for q in late:
            transpose_w(q)
        take_signs(late[0])

        out_view = out.rearrange("(cb r eb) n -> cb r eb n", r=P, eb=2)
        relu = {}
        normed = {}

        def relu_2(m, half):
            if half == 0:
                relu[m] = stage.tile([P, HALVES, BANK], F32, name="relu", bufs=6)
            nc.scalar.activation(out=relu[m][:, half, :], in_=sums[TILES + m, half][:], func=ACT.Relu)

        def normalise_2(m, half, engine):
            if half == 0:
                normed[m] = stage.tile([P, SIZE], F32, name="normed", bufs=5)
            values = normed[m][:, BANK * half : BANK * (half + 1)]
            factor, shift = factors[TILES + m][:, 0:1], coeff[TILES + m][:]
            if engine is nc.scalar:
                nc.scalar.activation(out=values, in_=relu[m][:, half, :], func=ACT.Identity, scale=factor, bias=shift)
            else:
                engine.tensor_scalar(
                    out=values, in0=relu[m][:, half, :], scalar1=factor, scalar2=shift, op0=ALU.mult, op1=ALU.add
                )

        blocks = {}

        def transpose_block(c, cb):
            blocks[c, cb] = psum.tile([P, BANK], F32, name="block", tag="bank")
            for eb in range(2):
                for e in range(2):
                    w = 2 * eb + e
                    nc.tensor.transpose(
                        blocks[c, cb][:, P * w : P * (w + 1)],
                        normed[2 * c + e][:, CHUNK * cb + P * eb : CHUNK * cb + P * (eb + 1)],
                        ident[:],
                    )

        def store_block(c, cb, copy):
            rows = stage.tile([P, 2, CHUNK], F32, tag="rows", bufs=8)
            copy(
                out=rows[:].rearrange("p eb (j e) -> p eb j e", e=2),
                in_=blocks[c, cb][:].rearrange("p (eb e j) -> p eb j e", eb=2, e=2),
            )
            nc.sync.dma_start(out=out_view[cb][:, :, CHUNK * c : CHUNK * (c + 1)], in_=rows[:])

        def chain(m):
            take_rstd(TILES + m)
            take_factors(TILES + m, nc.scalar)
            take_shift(TILES + m, nc.scalar)

        def norm(m, engine):
            for half in range(HALVES):
                normalise_2(m, half, engine)

        def two_blocks(c, cb):
            transpose_block(c, cb)
            transpose_block(c, cb + 1)

        def store_two(c, cb):
            store_block(c, cb, nc.scalar.copy)
            store_block(c, cb + 1, nc.vector.tensor_copy)

        for g in range(PASSES):
            for half in range(HALVES):
                for m in range(2):
                    product_pass(TILES + m, "h1", half, g)
        LAST = TILES - 1
        unquantised = scalar_plan[-1] + vector_plan[-1] + list(late)
        relu_2(0, 0)
        relu_2(1, 0)
        take_stats(TILES, 0, relu[0][:, 0, :])
        take_signs(late[1])
        relu_2(0, 1)
        for i in range(1, TILES):
            c, cb = (i - 5) // 2, 2 * ((i - 5) % 2)
            if i + 1 < TILES:
                for half in range(HALVES):
                    product(TILES + i + 1, "h1", half)
            if i >= 5:
                two_blocks(c, cb)
            if i > 1:
                relu_2(i, 0)
            if i >= 2:
                take_rstd(TILES + i - 2)
            relu_2(i, 1)
            if i >= 2:
                take_factors(TILES + i - 2, nc.scalar)
            take_stats(TILES + i - 1, 1, relu[i - 1][:, 1, :])
            take_stats(TILES + i, 0, relu[i][:, 0, :])
            aggregate(TILES + i - 1)
            if i <= len(unquantised):
                quantise_w(unquantised[i - 1])
            if i >= 5:
                store_two(c, cb)
            if i >= 2:
                take_shift(TILES + i - 2, nc.scalar)
                norm(i - 2, nc.gpsimd)
        take_rstd(TILES + LAST - 1)
        take_factors(TILES + LAST - 1, nc.scalar)
        take_stats(TILES + LAST, 1, relu[LAST][:, 1, :])
        two_blocks(1, 2)
        store_block(1, 2, nc.scalar.copy)
        take_shift(TILES + LAST - 1, nc.scalar)
        norm(LAST - 1, nc.gpsimd)
        aggregate(TILES + LAST)
        store_block(1, 3, nc.vector.tensor_copy)
        chain(LAST)
        two_blocks(2, 0)
        store_block(2, 0, nc.vector.tensor_copy)
        norm(LAST, nc.scalar)
        two_blocks(2, 2)
        store_block(2, 1, nc.vector.tensor_copy)
        store_block(2, 2, nc.vector.tensor_copy)
        store_block(2, 3, nc.scalar.copy)
        two_blocks(3, 0)
        two_blocks(3, 2)
        store_block(3, 0, nc.vector.tensor_copy)
        store_block(3, 1, nc.scalar.copy)
        store_block(3, 2, nc.vector.tensor_copy)
        store_block(3, 3, nc.scalar.copy)
